import numpy as np
import ml_dtypes


def mxq(x, axis, fmt="e4m3"):
    dtype, down = {"e4m3": (ml_dtypes.float8_e4m3fn, 7), "e5m2": (ml_dtypes.float8_e5m2, 14)}[fmt]
    v = np.moveaxis(np.asarray(x, np.float32).astype(ml_dtypes.bfloat16).astype(np.float64), axis, -1)
    blocks = v.reshape(v.shape[:-1] + (-1, 32))
    amax = np.abs(blocks).max(-1, keepdims=True)
    byte = np.maximum(np.where(amax > 0, np.frexp(amax)[1] - 1 + 127, 0) - down, 1)
    scale = np.exp2(byte - 127.0)
    codes = (blocks / scale).astype(np.float32).astype(dtype).astype(np.float64)
    return np.moveaxis((codes * scale).reshape(v.shape), -1, axis)


WIDE = False


def mx_kscale(k):
    if not WIDE:
        return np.ones(k)
    levels = np.array([10, -10, 5, -5, 0])
    a = np.random.permutation(np.resize(levels, k // 512 * 4)).reshape(k // 512, 4)
    idx = np.arange(k)
    return np.exp2(a[idx // 512, idx % 128 // 32])


BF16 = ml_dtypes.bfloat16


def bf(x):
    return np.asarray(x, np.float32).astype(BF16)


def f64(x):
    return np.asarray(x).astype(np.float64)


B, K, N = 4096, 512, 1024


def setup_inputs():
    s = mx_kscale(K)
    s = s / s.max()
    return {"x": bf(np.random.standard_normal((B, K)) * s),
            "W": bf(np.random.standard_normal((K, N)) * 0.4 / np.sqrt(K) / s[:, None]),
            "P": bf(np.random.standard_normal(N) * 0.3),
            "w": bf(0.8 + 0.1 * np.random.standard_normal(1)),
            "p": bf(0.5 + 0.1 * np.random.standard_normal(1)),
            "sine_w": bf(1.2 + 0.1 * np.random.standard_normal(1)),
            "cosine_w": bf(-0.7 + 0.1 * np.random.standard_normal(1))}


def reference(x, W, P, w, p, sine_w, cosine_w):
    x = f64(x)
    original = f64(w) * x + f64(p)
    z = (mxq(x, 1, "e4m3") @ mxq(f64(W), 0, "e4m3")) + f64(P)
    periodic = f64(sine_w) * np.sin(z) + f64(cosine_w) * np.cos(z)
    return np.concatenate((original, periodic), axis=-1)

@@ -1,0 +1,300 @@
+import math
+from contextlib import ExitStack
+
+import concourse.mybir as mybir
+from concourse.masks import make_identity
+
+FLOPS = 2 * 4096 * 512 * 1024
+
+F32 = mybir.dt.float32
+BF16 = mybir.dt.bfloat16
+I32 = mybir.dt.int32
+U32 = mybir.dt.uint32
+U8 = mybir.dt.uint8
+FP8X4 = mybir.dt.float8_e4m3fn_x4
+ALU = mybir.AluOpType
+ACT = mybir.ActivationFunctionType
+
+PIN = False
+NP = 128
+BLOCKS = 8
+NT = 8
+STEPS = BLOCKS * NT
+TWO_PI = 2.0 * math.pi
+HALF_PI = 0.5 * math.pi
+TINY = 1.0e-30
+STORE_AFTER = {False: {3: 0, 7: 4}, True: {3: 0, 5: 4, 6: 6, 7: 7}}
+AHEAD = 2
+
+
+def tile_time2vec_t_kernel(tc, x, W, P, w, p, sine_w, cosine_w, out):
+    nc = tc.nc
+    with ExitStack() as ctx:
+        keep = ctx.enter_context(tc.tile_pool(name="keep", bufs=1))
+        xq = ctx.enter_context(tc.tile_pool(name="xq", bufs=2))
+        work = ctx.enter_context(tc.tile_pool(name="work", bufs=3))
+        outp = ctx.enter_context(tc.tile_pool(name="outp", bufs=3))
+        ps_x = ctx.enter_context(tc.psum_pool(name="ps_x", bufs=2))
+        ps_z = ctx.enter_context(tc.psum_pool(name="ps_z", bufs=3))
+        ps_o = ctx.enter_context(tc.psum_pool(name="ps_o", bufs=3))
+
+        x_v = x.rearrange("(g p j) k -> g p j k", p=NP, j=4)
+        out_v = out.rearrange("(g p j) m -> g p j m", p=NP, j=4)
+        w_v = W.rearrange("(p j) n -> p j n", j=4)
+
+        c_bf = keep.tile([NP, 1], BF16, name="c_bf")
+        s_bf = keep.tile([NP, 1], BF16, name="s_bf")
+        w_bf = keep.tile([NP, 1], BF16, name="w_bf")
+        p_bf = keep.tile([NP, 1], BF16, name="p_bf")
+        p_rows = keep.tile([NP, NP], BF16, name="p_rows")
+        warm = keep.tile([NP, 1], F32, name="warm")
+        nc.vector.memset(warm[:], 0.0)
+        nc.vector.memset(p_rows[:], 0.0)
+
+        nc.scalar.dma_start(out=c_bf[:], in_=cosine_w.partition_broadcast(NP))
+        nc.scalar.dma_start(out=s_bf[:], in_=sine_w.partition_broadcast(NP))
+        nc.scalar.dma_start(out=p_rows[0:8, :], in_=P.rearrange("(t n) -> t n", n=NP))
+        nc.scalar.dma_start(out=w_bf[:], in_=w.partition_broadcast(NP))
+        nc.scalar.dma_start(out=p_bf[:], in_=p.partition_broadcast(NP))
+
+        x_sb = [keep.tile([NP, 4, 512], BF16, name="x_sb%d" % g) for g in range(BLOCKS)]
+        w_raw = keep.tile([NP, 4, 1024], BF16, name="w_raw")
+        nc.sync.dma_start(out=x_sb[0][:], in_=x_v[0])
+        nc.sync.dma_start(out=w_raw[:, :, 0:512], in_=w_v[:, :, 0:512])
+        nc.sync.dma_start(out=x_sb[1][:], in_=x_v[1])
+        nc.sync.dma_start(out=w_raw[:, :, 512:1024], in_=w_v[:, :, 512:1024])
+        for g in range(2, BLOCKS):
+            nc.sync.dma_start(out=x_sb[g][:], in_=x_v[g])
+
+        warm2 = keep.tile([NP, 1], F32, name="warm2")
+        nc.scalar.activation(out=warm2[:], in_=warm[:], func=ACT.Sin)
+
+        ident = keep.tile([NP, NP], F32, name="ident")
+        make_identity(nc, ident[:])
+
+        sc = keep.tile([NP, 32], F32, name="sc")
+        trig = keep.tile([NP, 2], F32, name="trig")
+        beta = keep.tile([NP, NT], F32, name="beta")
+        bturn = keep.tile([NP, NT], F32, name="bturn")
+
+        def col(i):
+            return sc[:, i : i + 1]
+
+        (C_ABS, S_ABS, HS, S32, DD, RD, QQ, TH0, T1, T2, NUM, DEN, RDEN, TT, W2, W4, A1, A2, HH, TH, PHI,
+         G1, G2, G3, AMP, W32, P32) = range(27)
+
+        def ts(o, i, s1, s2, op0, op1):
+            nc.vector.tensor_scalar(out=o, in0=i, scalar1=s1, scalar2=s2, op0=op0, op1=op1)
+
+        def stt(o, i0, s, i1, op0, op1):
+            nc.vector.scalar_tensor_tensor(out=o, in0=i0, scalar=s, in1=i1, op0=op0, op1=op1)
+
+        stt(col(C_ABS), c_bf[:], -1.0, c_bf[:], ALU.mult, ALU.max)
+        stt(col(S_ABS), s_bf[:], -1.0, s_bf[:], ALU.mult, ALU.max)
+        nc.vector.tensor_copy(out=col(S32), in_=s_bf[:])
+        ts(col(HS), c_bf[:], 0.0, 0.5, ALU.is_ge, ALU.subtract)
+        stt(col(DD), col(S_ABS), TINY, col(C_ABS), ALU.max, ALU.add)
+        nc.vector.reciprocal(out=col(RD), in_=col(DD))
+        nc.vector.tensor_tensor(out=col(QQ), in0=col(S32), in1=col(RD), op=ALU.mult)
+        ts(col(TH0), col(QQ), -HALF_PI, HALF_PI, ALU.mult, ALU.add)
+        nc.scalar.activation(out=trig[:, 1:2], in_=col(QQ), func=ACT.Sin, scale=HALF_PI)
+        nc.scalar.activation(out=trig[:, 0:1], in_=col(TH0), func=ACT.Sin)
+        sn = trig[:, 0:1]
+        cs = trig[:, 1:2]
+
+        p_f32 = keep.tile([NP, NP], F32, name="p_f32")
+        nc.vector.tensor_copy(out=p_f32[:], in_=p_rows[:])
+        p_t = ps_x.tile([NP, NP], F32, name="p_t", tag="xt")
+        nc.tensor.transpose(p_t[:], p_f32[:], ident[:])
+
+        ts(col(T1), sn, col(S32), None, ALU.mult, ALU.bypass)
+        ts(col(T2), sn, col(C_ABS), TINY, ALU.mult, ALU.max)
+        stt(col(NUM), cs, col(C_ABS), col(T1), ALU.mult, ALU.subtract)
+        stt(col(DEN), cs, col(S32), col(T2), ALU.mult, ALU.add)
+        nc.vector.reciprocal(out=col(RDEN), in_=col(DEN))
+        nc.vector.tensor_tensor(out=col(TT), in0=col(NUM), in1=col(RDEN), op=ALU.mult)
+        nc.vector.tensor_tensor(out=col(W2), in0=col(TT), in1=col(TT), op=ALU.mult)
+        ts(col(A1), col(W2), -1.0 / 3.0, 1.0, ALU.mult, ALU.add)
+        ts(col(A2), col(W2), -1.0 / 7.0, 0.2, ALU.mult, ALU.add)
+        nc.vector.tensor_tensor(out=col(W4), in0=col(W2), in1=col(W2), op=ALU.mult)
+        ts(col(HH), col(A2), col(W4), col(A1), ALU.mult, ALU.add)
+        ts(col(TH), col(HH), col(TT), col(TH0), ALU.mult, ALU.add)
+        ts(col(PHI), col(TH), col(HS), 2.0, ALU.mult, ALU.mult)
+        ts(bturn[:], p_t[:, 0:NT], col(PHI), 1.0 / TWO_PI, ALU.add, ALU.mult)
+        ts(beta[:], p_t[:, 0:NT], col(PHI), None, ALU.add, ALU.bypass)
+        ts(col(G1), col(W2), 1.0 / 16.0, -0.125, ALU.mult, ALU.add)
+        ts(col(G2), col(G1), col(W2), 0.5, ALU.mult, ALU.add)
+        ts(col(G3), col(G2), col(W2), 1.0, ALU.mult, ALU.add)
+        nc.vector.tensor_tensor(out=col(AMP), in0=col(G3), in1=col(DEN), op=ALU.mult)
+        nc.vector.tensor_copy(out=col(W32), in_=w_bf[:])
+        nc.vector.tensor_copy(out=col(P32), in_=p_bf[:])
+
+        w_grp = keep.tile([NP, 1024, 4], BF16, name="w_grp", align_bytes=64)
+        w_code = keep.tile([NP, 1024], U32, name="w_code", align_bytes=64)
+        w_scale = keep.tile([NP, 1024], U8, name="w_scale", align_bytes=64)
+
+        def w_regroup(q, on_vector):
+            cols = slice(q * 256, (q + 1) * 256)
+            dst = w_grp[:, cols, :].rearrange("p (c i) t -> p c t i", i=4)
+            src = w_raw[:, :, cols].rearrange("p t (c i) -> p c t i", i=4)
+            if on_vector:
+                nc.vector.tensor_copy(out=dst, in_=src)
+            else:
+                nc.scalar.copy(out=dst, in_=src)
+
+        def w_quant(q):
+            cols = slice(q * 256, (q + 1) * 256)
+            nc.vector.quantize_mx(
+                out=w_code[:, cols].bitcast(FP8X4),
+                scales=w_scale[:, cols],
+                in_=w_grp[:, cols, :].rearrange("p c t -> p (c t)"),
+            )
+
+        xt_of = {}
+        grp_of = {}
+        code_of = {}
+        scale_of = {}
+
+        def x_transposes(g):
+            words = x_sb[g][:].bitcast(F32).rearrange("p j (q u) -> p j q u", u=2)
+            for h in range(2):
+                xt = ps_x.tile([NP, 2, 256], F32, name="xt", tag="xt")
+                xt_of[(g, h)] = xt
+                for jj in range(2):
+                    for u in range(2):
+                        nc.tensor.transpose(
+                            xt[:, u, jj * NP : (jj + 1) * NP], words[:, 2 * h + jj, :, u], ident[:]
+                        )
+
+        def x_exit(g, h, on_vector):
+            if h == 0:
+                grp = xq.tile([NP, 512, 4], BF16, name="grp", align_bytes=64)
+                grp_of[g] = grp
+            dst = grp_of[g][:].bitcast(F32)[:, h * 256 : (h + 1) * 256, :]
+            src = xt_of[(g, h)][:].rearrange("p u c -> p c u")
+            if on_vector:
+                nc.vector.tensor_copy(out=dst, in_=src)
+            else:
+                nc.scalar.copy(out=dst, in_=src)
+
+        def x_quant(g):
+            code = keep.tile([NP, 512], U32, name="code%d" % g, align_bytes=64)
+            scale = keep.tile([NP, 512], U8, name="scale%d" % g, align_bytes=64)
+            code_of[g] = code
+            scale_of[g] = scale
+            nc.vector.quantize_mx(
+                out=code[:].bitcast(FP8X4),
+                scales=scale[:],
+                in_=grp_of[g][:].rearrange("p c t -> p (c t)"),
+            )
+
+        z_of = {}
+        k_of = {}
+        r_of = {}
+        s_of = {}
+        o_of = {}
+        ot_of = {}
+
+        def mx(s):
+            g, nt = divmod(s, NT)
+            z = ps_z.tile([NP, 512], F32, name="z")
+            z_of[s] = z
+            cols = slice(nt * NP, (nt + 1) * NP)
+            nc.tensor.matmul_mx(
+                out=z[:],
+                lhsT=w_code[:, cols].bitcast(FP8X4),
+                lhsT_scale=w_scale[:, cols],
+                rhs=code_of[g][:].bitcast(FP8X4),
+                rhs_scale=scale_of[g][:],
+                start=True,
+                stop=True,
+            )
+
+        def vk(s):
+            nt = s % NT
+            kt = work.tile([NP, 512], I32, name="kt")
+            k_of[s] = kt
+            ts(kt[:], z_of[s][:], 1.0 / TWO_PI, bturn[:, nt : nt + 1], ALU.mult, ALU.add)
+
+        def vr(s):
+            rt = work.tile([NP, 512], F32, name="rt", bufs=6)
+            r_of[s] = rt
+            stt(rt[:], k_of[s][:], -TWO_PI, z_of[s][:], ALU.mult, ALU.add)
+
+        def sine(s):
+            nt = s % NT
+            st = work.tile([NP, 512], F32, name="st", bufs=4)
+            s_of[s] = st
+            nc.scalar.activation(out=st[:], in_=r_of[s][:], func=ACT.Sin, bias=beta[:, nt : nt + 1], scale=1.0)
+
+        def tr(s):
+            o = ps_o.tile([NP, 512], F32, name="o")
+            o_of[s] = o
+            for j in range(4):
+                nc.tensor.transpose(o[:, j * NP : (j + 1) * NP], s_of[s][:, j * NP : (j + 1) * NP], ident[:])
+
+        def ex(s, on_vector):
+            g, nt = divmod(s, NT)
+            dst = ot_of[g][:, :, 512 + nt * NP : 512 + (nt + 1) * NP]
+            src = o_of[s][:].rearrange("p (j n) -> p j n", j=4)
+            if on_vector:
+                nc.vector.tensor_scalar(out=dst, in0=src, scalar1=col(AMP), scalar2=None, op0=ALU.mult)
+            else:
+                nc.scalar.activation(out=dst, in_=src, func=ACT.Copy, scale=col(AMP))
+            first = STORE_AFTER[g == BLOCKS - 1].get(nt)
+            if first is not None:
+                cols = slice(512 + first * NP, 512 + (nt + 1) * NP)
+                nc.sync.dma_start(out=out_v[g][:, :, cols], in_=ot_of[g][:, :, cols])
+
+        def lin(g):
+            ot = outp.tile([NP, 4, 1536], F32, name="ot")
+            ot_of[g] = ot
+            nc.gpsimd.tensor_scalar(
+                out=ot[:, :, 0:512], in0=x_sb[g][:], scalar1=col(W32), scalar2=col(P32), op0=ALU.mult, op1=ALU.add
+            )
+            nc.sync.dma_start(out=out_v[g][:, :, 0:512], in_=ot[:, :, 0:512])
+
+        x_transposes(0)
+        w_regroup(0, True)
+        w_regroup(1, False)
+        x_exit(0, 0, False)
+        x_exit(0, 1, True)
+        w_quant(0)
+        x_quant(0)
+        w_quant(1)
+        w_regroup(2, True)
+        w_regroup(3, False)
+        w_quant(2)
+        w_quant(3)
+        x_transposes(1)
+        x_exit(1, 0, False)
+        x_exit(1, 1, True)
+        x_quant(1)
+
+        if PIN:
+            ctx.enter_context(tc.manual_schedule())
+
+        for t in range(STEPS + 5):
+            g, nt = divmod(t, NT)
+            if t < STEPS:
+                if nt == 0:
+                    lin(g)
+                mx(t)
+            if 0 <= t - 1 < STEPS:
+                vk(t - 1)
+            if 0 <= t - 2 < STEPS:
+                vr(t - 2)
+            if 0 <= t - 3 < STEPS:
+                sine(t - 3)
+            if 0 <= t - 4 < STEPS:
+                tr(t - 4)
+            if g + AHEAD < BLOCKS:
+                if nt == 2:
+                    x_transposes(g + AHEAD)
+                if nt == 3:
+                    x_exit(g + AHEAD, 0, False)
+                    x_exit(g + AHEAD, 1, True)
+                if nt == 5:
+                    x_quant(g + AHEAD)
+            if 0 <= t - 5 < STEPS:
+                ex(t - 5, t - 5 >= STEPS - 2)

@@ -15,7 +15,6 @@ FP8X4 = mybir.dt.float8_e4m3fn_x4
 ALU = mybir.AluOpType
 ACT = mybir.ActivationFunctionType
 
-PIN = False
 NP = 128
 BLOCKS = 8
 NT = 8
@@ -24,7 +23,10 @@ TWO_PI = 2.0 * math.pi
 HALF_PI = 0.5 * math.pi
 TINY = 1.0e-30
 STORE_AFTER = {False: {3: 0, 7: 4}, True: {3: 0, 5: 4, 6: 6, 7: 7}}
-AHEAD = 2
+GROUP = 4
+GROUPS = STEPS // GROUP
+X_LEAD = 5
+EXIT_ON_VECTOR = (56, 57, 58, 59, 62)
 
 
 def tile_time2vec_t_kernel(tc, x, W, P, w, p, sine_w, cosine_w, out):
@@ -34,9 +36,9 @@ def tile_time2vec_t_kernel(tc, x, W, P, w, p, sine_w, cosine_w, out):
         xq = ctx.enter_context(tc.tile_pool(name="xq", bufs=2))
         work = ctx.enter_context(tc.tile_pool(name="work", bufs=3))
         outp = ctx.enter_context(tc.tile_pool(name="outp", bufs=3))
-        ps_x = ctx.enter_context(tc.psum_pool(name="ps_x", bufs=2))
-        ps_z = ctx.enter_context(tc.psum_pool(name="ps_z", bufs=3))
-        ps_o = ctx.enter_context(tc.psum_pool(name="ps_o", bufs=3))
+        ps_z = ctx.enter_context(tc.psum_pool(name="ps_z", bufs=4))
+        ps_o = ctx.enter_context(tc.psum_pool(name="ps_o", bufs=4))
+        ctx.enter_context(tc.manual_schedule())
 
         x_v = x.rearrange("(g p j) k -> g p j k", p=NP, j=4)
         out_v = out.rearrange("(g p j) m -> g p j m", p=NP, j=4)
@@ -48,6 +50,7 @@ def tile_time2vec_t_kernel(tc, x, W, P, w, p, sine_w, cosine_w, out):
         p_bf = keep.tile([NP, 1], BF16, name="p_bf")
         p_rows = keep.tile([NP, NP], BF16, name="p_rows")
         warm = keep.tile([NP, 1], F32, name="warm")
+        warm2 = keep.tile([NP, 1], F32, name="warm2")
         nc.vector.memset(warm[:], 0.0)
         nc.vector.memset(p_rows[:], 0.0)
 
@@ -61,12 +64,10 @@ def tile_time2vec_t_kernel(tc, x, W, P, w, p, sine_w, cosine_w, out):
         w_raw = keep.tile([NP, 4, 1024], BF16, name="w_raw")
         nc.sync.dma_start(out=x_sb[0][:], in_=x_v[0])
         nc.sync.dma_start(out=w_raw[:, :, 0:512], in_=w_v[:, :, 0:512])
-        nc.sync.dma_start(out=x_sb[1][:], in_=x_v[1])
         nc.sync.dma_start(out=w_raw[:, :, 512:1024], in_=w_v[:, :, 512:1024])
-        for g in range(2, BLOCKS):
+        for g in range(1, BLOCKS):
             nc.sync.dma_start(out=x_sb[g][:], in_=x_v[g])
 
-        warm2 = keep.tile([NP, 1], F32, name="warm2")
         nc.scalar.activation(out=warm2[:], in_=warm[:], func=ACT.Sin)
 
         ident = keep.tile([NP, NP], F32, name="ident")
@@ -76,6 +77,9 @@ def tile_time2vec_t_kernel(tc, x, W, P, w, p, sine_w, cosine_w, out):
         trig = keep.tile([NP, 2], F32, name="trig")
         beta = keep.tile([NP, NT], F32, name="beta")
         bturn = keep.tile([NP, NT], F32, name="bturn")
+        p_f32 = keep.tile([NP, NP], F32, name="p_f32")
+        sn = trig[:, 0:1]
+        cs = trig[:, 1:2]
 
         def col(i):
             return sc[:, i : i + 1]
@@ -89,45 +93,8 @@ def tile_time2vec_t_kernel(tc, x, W, P, w, p, sine_w, cosine_w, out):
         def stt(o, i0, s, i1, op0, op1):
             nc.vector.scalar_tensor_tensor(out=o, in0=i0, scalar=s, in1=i1, op0=op0, op1=op1)
 
-        stt(col(C_ABS), c_bf[:], -1.0, c_bf[:], ALU.mult, ALU.max)
-        stt(col(S_ABS), s_bf[:], -1.0, s_bf[:], ALU.mult, ALU.max)
-        nc.vector.tensor_copy(out=col(S32), in_=s_bf[:])
-        ts(col(HS), c_bf[:], 0.0, 0.5, ALU.is_ge, ALU.subtract)
-        stt(col(DD), col(S_ABS), TINY, col(C_ABS), ALU.max, ALU.add)
-        nc.vector.reciprocal(out=col(RD), in_=col(DD))
-        nc.vector.tensor_tensor(out=col(QQ), in0=col(S32), in1=col(RD), op=ALU.mult)
-        ts(col(TH0), col(QQ), -HALF_PI, HALF_PI, ALU.mult, ALU.add)
-        nc.scalar.activation(out=trig[:, 1:2], in_=col(QQ), func=ACT.Sin, scale=HALF_PI)
-        nc.scalar.activation(out=trig[:, 0:1], in_=col(TH0), func=ACT.Sin)
-        sn = trig[:, 0:1]
-        cs = trig[:, 1:2]
-
-        p_f32 = keep.tile([NP, NP], F32, name="p_f32")
-        nc.vector.tensor_copy(out=p_f32[:], in_=p_rows[:])
-        p_t = ps_x.tile([NP, NP], F32, name="p_t", tag="xt")
-        nc.tensor.transpose(p_t[:], p_f32[:], ident[:])
-
-        ts(col(T1), sn, col(S32), None, ALU.mult, ALU.bypass)
-        ts(col(T2), sn, col(C_ABS), TINY, ALU.mult, ALU.max)
-        stt(col(NUM), cs, col(C_ABS), col(T1), ALU.mult, ALU.subtract)
-        stt(col(DEN), cs, col(S32), col(T2), ALU.mult, ALU.add)
-        nc.vector.reciprocal(out=col(RDEN), in_=col(DEN))
-        nc.vector.tensor_tensor(out=col(TT), in0=col(NUM), in1=col(RDEN), op=ALU.mult)
-        nc.vector.tensor_tensor(out=col(W2), in0=col(TT), in1=col(TT), op=ALU.mult)
-        ts(col(A1), col(W2), -1.0 / 3.0, 1.0, ALU.mult, ALU.add)
-        ts(col(A2), col(W2), -1.0 / 7.0, 0.2, ALU.mult, ALU.add)
-        nc.vector.tensor_tensor(out=col(W4), in0=col(W2), in1=col(W2), op=ALU.mult)
-        ts(col(HH), col(A2), col(W4), col(A1), ALU.mult, ALU.add)
-        ts(col(TH), col(HH), col(TT), col(TH0), ALU.mult, ALU.add)
-        ts(col(PHI), col(TH), col(HS), 2.0, ALU.mult, ALU.mult)
-        ts(bturn[:], p_t[:, 0:NT], col(PHI), 1.0 / TWO_PI, ALU.add, ALU.mult)
-        ts(beta[:], p_t[:, 0:NT], col(PHI), None, ALU.add, ALU.bypass)
-        ts(col(G1), col(W2), 1.0 / 16.0, -0.125, ALU.mult, ALU.add)
-        ts(col(G2), col(G1), col(W2), 0.5, ALU.mult, ALU.add)
-        ts(col(G3), col(G2), col(W2), 1.0, ALU.mult, ALU.add)
-        nc.vector.tensor_tensor(out=col(AMP), in0=col(G3), in1=col(DEN), op=ALU.mult)
-        nc.vector.tensor_copy(out=col(W32), in_=w_bf[:])
-        nc.vector.tensor_copy(out=col(P32), in_=p_bf[:])
+        def tt(o, i0, i1):
+            nc.vector.tensor_tensor(out=o, in0=i0, in1=i1, op=ALU.mult)
 
         w_grp = keep.tile([NP, 1024, 4], BF16, name="w_grp", align_bytes=64)
         w_code = keep.tile([NP, 1024], U32, name="w_code", align_bytes=64)
@@ -155,16 +122,16 @@ def tile_time2vec_t_kernel(tc, x, W, P, w, p, sine_w, cosine_w, out):
         code_of = {}
         scale_of = {}
 
-        def x_transposes(g):
+        def x_transposes(g, h, in_o_ring):
             words = x_sb[g][:].bitcast(F32).rearrange("p j (q u) -> p j q u", u=2)
-            for h in range(2):
-                xt = ps_x.tile([NP, 2, 256], F32, name="xt", tag="xt")
-                xt_of[(g, h)] = xt
-                for jj in range(2):
-                    for u in range(2):
-                        nc.tensor.transpose(
-                            xt[:, u, jj * NP : (jj + 1) * NP], words[:, 2 * h + jj, :, u], ident[:]
-                        )
+            if in_o_ring:
+                xt = ps_o.tile([NP, 2, 256], F32, name="xt_o", tag="o")
+            else:
+                xt = ps_z.tile([NP, 2, 256], F32, name="xt_z", tag="z")
+            xt_of[(g, h)] = xt
+            for jj in range(2):
+                for u in range(2):
+                    nc.tensor.transpose(xt[:, u, jj * NP : (jj + 1) * NP], words[:, 2 * h + jj, :, u], ident[:])
 
         def x_exit(g, h, on_vector):
             if h == 0:
@@ -197,7 +164,7 @@ def tile_time2vec_t_kernel(tc, x, W, P, w, p, sine_w, cosine_w, out):
 
         def mx(s):
             g, nt = divmod(s, NT)
-            z = ps_z.tile([NP, 512], F32, name="z")
+            z = ps_z.tile([NP, 512], F32, name="z", tag="z")
             z_of[s] = z
             cols = slice(nt * NP, (nt + 1) * NP)
             nc.tensor.matmul_mx(
@@ -217,18 +184,18 @@ def tile_time2vec_t_kernel(tc, x, W, P, w, p, sine_w, cosine_w, out):
             ts(kt[:], z_of[s][:], 1.0 / TWO_PI, bturn[:, nt : nt + 1], ALU.mult, ALU.add)
 
         def vr(s):
-            rt = work.tile([NP, 512], F32, name="rt", bufs=6)
+            rt = work.tile([NP, 512], F32, name="rt", bufs=8)
             r_of[s] = rt
             stt(rt[:], k_of[s][:], -TWO_PI, z_of[s][:], ALU.mult, ALU.add)
 
         def sine(s):
             nt = s % NT
-            st = work.tile([NP, 512], F32, name="st", bufs=4)
+            st = work.tile([NP, 512], F32, name="st", bufs=8)
             s_of[s] = st
             nc.scalar.activation(out=st[:], in_=r_of[s][:], func=ACT.Sin, bias=beta[:, nt : nt + 1], scale=1.0)
 
         def tr(s):
-            o = ps_o.tile([NP, 512], F32, name="o")
+            o = ps_o.tile([NP, 512], F32, name="o", tag="o")
             o_of[s] = o
             for j in range(4):
                 nc.tensor.transpose(o[:, j * NP : (j + 1) * NP], s_of[s][:, j * NP : (j + 1) * NP], ident[:])
@@ -254,47 +221,87 @@ def tile_time2vec_t_kernel(tc, x, W, P, w, p, sine_w, cosine_w, out):
             )
             nc.sync.dma_start(out=out_v[g][:, :, 0:512], in_=ot[:, :, 0:512])
 
-        x_transposes(0)
-        w_regroup(0, True)
-        w_regroup(1, False)
+        stt(col(C_ABS), c_bf[:], -1.0, c_bf[:], ALU.mult, ALU.max)
+        stt(col(S_ABS), s_bf[:], -1.0, s_bf[:], ALU.mult, ALU.max)
+        nc.vector.tensor_copy(out=col(S32), in_=s_bf[:])
+        stt(col(DD), col(S_ABS), TINY, col(C_ABS), ALU.max, ALU.add)
+        ts(col(HS), c_bf[:], 0.0, 0.5, ALU.is_ge, ALU.subtract)
+        nc.vector.reciprocal(out=col(RD), in_=col(DD))
+        tt(col(QQ), col(S32), col(RD))
+        ts(col(TH0), col(QQ), -HALF_PI, HALF_PI, ALU.mult, ALU.add)
+        nc.scalar.activation(out=cs, in_=col(QQ), func=ACT.Sin, scale=HALF_PI)
+        nc.scalar.activation(out=sn, in_=col(TH0), func=ACT.Sin)
+        nc.vector.tensor_copy(out=p_f32[:], in_=p_rows[:])
+        nc.vector.tensor_copy(out=col(W32), in_=w_bf[:])
+        nc.vector.tensor_copy(out=col(P32), in_=p_bf[:])
+
+        x_transposes(0, 0, True)
+        x_transposes(0, 1, True)
+        p_t = ps_o.tile([NP, NP], F32, name="p_t", tag="o")
+        nc.tensor.transpose(p_t[:], p_f32[:], ident[:])
         x_exit(0, 0, False)
-        x_exit(0, 1, True)
+        x_exit(0, 1, False)
+
+        ts(col(T1), sn, col(S32), None, ALU.mult, ALU.bypass)
+        ts(col(T2), sn, col(C_ABS), TINY, ALU.mult, ALU.max)
+        stt(col(NUM), cs, col(C_ABS), col(T1), ALU.mult, ALU.subtract)
+        stt(col(DEN), cs, col(S32), col(T2), ALU.mult, ALU.add)
+        nc.vector.reciprocal(out=col(RDEN), in_=col(DEN))
+        tt(col(TT), col(NUM), col(RDEN))
+        tt(col(W2), col(TT), col(TT))
+        w_regroup(0, True)
+        ts(col(A1), col(W2), -1.0 / 3.0, 1.0, ALU.mult, ALU.add)
+        ts(col(A2), col(W2), -1.0 / 7.0, 0.2, ALU.mult, ALU.add)
+        tt(col(W4), col(W2), col(W2))
+        ts(col(HH), col(A2), col(W4), col(A1), ALU.mult, ALU.add)
+        ts(col(TH), col(HH), col(TT), col(TH0), ALU.mult, ALU.add)
+        ts(col(PHI), col(TH), col(HS), 2.0, ALU.mult, ALU.mult)
+        ts(bturn[:], p_t[:, 0:NT], col(PHI), 1.0 / TWO_PI, ALU.add, ALU.mult)
+        ts(beta[:], p_t[:, 0:NT], col(PHI), None, ALU.add, ALU.bypass)
         w_quant(0)
         x_quant(0)
+        for q in range(1, 4):
+            w_regroup(q, False)
         w_quant(1)
-        w_regroup(2, True)
-        w_regroup(3, False)
-        w_quant(2)
-        w_quant(3)
-        x_transposes(1)
-        x_exit(1, 0, False)
-        x_exit(1, 1, True)
-        x_quant(1)
 
-        if PIN:
-            ctx.enter_context(tc.manual_schedule())
-
-        for t in range(STEPS + 5):
-            g, nt = divmod(t, NT)
-            if t < STEPS:
-                if nt == 0:
-                    lin(g)
-                mx(t)
-            if 0 <= t - 1 < STEPS:
-                vk(t - 1)
-            if 0 <= t - 2 < STEPS:
-                vr(t - 2)
-            if 0 <= t - 3 < STEPS:
-                sine(t - 3)
-            if 0 <= t - 4 < STEPS:
-                tr(t - 4)
-            if g + AHEAD < BLOCKS:
-                if nt == 2:
-                    x_transposes(g + AHEAD)
-                if nt == 3:
-                    x_exit(g + AHEAD, 0, False)
-                    x_exit(g + AHEAD, 1, True)
-                if nt == 5:
-                    x_quant(g + AHEAD)
-            if 0 <= t - 5 < STEPS:
-                ex(t - 5, t - 5 >= STEPS - 2)
+        for i in range(-1, GROUPS + 1):
+            if i % 2 == 1 and (i + 1) // 2 < BLOCKS:
+                lin((i + 1) // 2)
+            steps = [s for s in range(GROUP * i + 3, GROUP * i + 7) if 0 <= s < STEPS]
+            for s in steps:
+                mx(s)
+            for s in steps:
+                vk(s)
+                if s >= 1:
+                    vr(s - 1)
+                if s == 0:
+                    ts(col(G1), col(W2), 1.0 / 16.0, -0.125, ALU.mult, ALU.add)
+                    ts(col(G2), col(G1), col(W2), 0.5, ALU.mult, ALU.add)
+                    ts(col(G3), col(G2), col(W2), 1.0, ALU.mult, ALU.add)
+                    tt(col(AMP), col(G3), col(DEN))
+                if s == 1:
+                    w_quant(2)
+                if s == 2:
+                    w_quant(3)
+            if i == GROUPS - 1:
+                vr(STEPS - 1)
+            if i == 0:
+                x_quant(1)
+            if i >= 1 and i % 2 == 1 and (i + 3) // 2 < BLOCKS:
+                x_quant((i + 3) // 2)
+            if 0 <= i < GROUPS:
+                for s in range(GROUP * i, GROUP * i + GROUP):
+                    sine(s)
+            halves = [i + X_LEAD] if i + X_LEAD < 2 * BLOCKS else []
+            if i == -1:
+                halves = [2, 3, 4]
+            for xi in halves:
+                x_transposes(xi // 2, xi % 2, xi < 4)
+            if i >= 1:
+                for s in range(GROUP * (i - 1), GROUP * i):
+                    tr(s)
+            for xi in halves:
+                x_exit(xi // 2, xi % 2, False)
+            if i >= 1:
+                for s in range(GROUP * (i - 1), GROUP * i):
+                    ex(s, s in EXIT_ON_VECTOR)

@@ -167,15 +167,16 @@ def tile_time2vec_t_kernel(tc, x, W, P, w, p, sine_w, cosine_w, out):
             z = ps_z.tile([NP, 512], F32, name="z", tag="z")
             z_of[s] = z
             cols = slice(nt * NP, (nt + 1) * NP)
-            nc.tensor.matmul_mx(
-                out=z[:],
-                lhsT=w_code[:, cols].bitcast(FP8X4),
-                lhsT_scale=w_scale[:, cols],
-                rhs=code_of[g][:].bitcast(FP8X4),
-                rhs_scale=scale_of[g][:],
-                start=True,
-                stop=True,
-            )
+            for rep_ in range(2):
+                nc.tensor.matmul_mx(
+                    out=z[:],
+                    lhsT=w_code[:, cols].bitcast(FP8X4),
+                    lhsT_scale=w_scale[:, cols],
+                    rhs=code_of[g][:].bitcast(FP8X4),
+                    rhs_scale=scale_of[g][:],
+                    start=True,
+                    stop=True,
+                )
 
         def vk(s):
             nt = s % NT

@@ -34,10 +34,17 @@ def tile_time2vec_t_kernel(tc, x, W, P, w, p, sine_w, cosine_w, out):
     with ExitStack() as ctx:
         keep = ctx.enter_context(tc.tile_pool(name="keep", bufs=1))
         xq = ctx.enter_context(tc.tile_pool(name="xq", bufs=2))
-        work = ctx.enter_context(tc.tile_pool(name="work", bufs=3))
         outp = ctx.enter_context(tc.tile_pool(name="outp", bufs=3))
-        ps_z = ctx.enter_context(tc.psum_pool(name="ps_z", bufs=4))
-        ps_o = ctx.enter_context(tc.psum_pool(name="ps_o", bufs=4))
+        ps_z = ctx.enter_context(tc.psum_pool(name="ps_z", bufs=1))
+        ps_o = ctx.enter_context(tc.psum_pool(name="ps_o", bufs=1))
+        ring = ctx.enter_context(tc.tile_pool(name="ring", bufs=1))
+        turn = {"z": 0, "o": 0, "kt": 0, "rt": 0, "st": 0}
+
+        def slot(kind, size):
+            n = turn[kind]
+            turn[kind] = n + 1
+            return "%s%d" % (kind, n % size)
+
         ctx.enter_context(tc.manual_schedule())
 
         x_v = x.rearrange("(g p j) k -> g p j k", p=NP, j=4)
@@ -125,9 +132,9 @@ def tile_time2vec_t_kernel(tc, x, W, P, w, p, sine_w, cosine_w, out):
         def x_transposes(g, h, in_o_ring):
             words = x_sb[g][:].bitcast(F32).rearrange("p j (q u) -> p j q u", u=2)
             if in_o_ring:
-                xt = ps_o.tile([NP, 2, 256], F32, name="xt_o", tag="o")
+                xt = ps_o.tile([NP, 2, 256], F32, name="xt_o", tag=slot("o", 4))
             else:
-                xt = ps_z.tile([NP, 2, 256], F32, name="xt_z", tag="z")
+                xt = ps_z.tile([NP, 2, 256], F32, name="xt_z", tag=slot("z", 4))
             xt_of[(g, h)] = xt
             for jj in range(2):
                 for u in range(2):
@@ -164,39 +171,38 @@ def tile_time2vec_t_kernel(tc, x, W, P, w, p, sine_w, cosine_w, out):
 
         def mx(s):
             g, nt = divmod(s, NT)
-            z = ps_z.tile([NP, 512], F32, name="z", tag="z")
+            z = ps_z.tile([NP, 512], F32, name="z", tag=slot("z", 4))
             z_of[s] = z
             cols = slice(nt * NP, (nt + 1) * NP)
-            for rep_ in range(2):
-                nc.tensor.matmul_mx(
-                    out=z[:],
-                    lhsT=w_code[:, cols].bitcast(FP8X4),
-                    lhsT_scale=w_scale[:, cols],
-                    rhs=code_of[g][:].bitcast(FP8X4),
-                    rhs_scale=scale_of[g][:],
-                    start=True,
-                    stop=True,
-                )
+            nc.tensor.matmul_mx(
+                out=z[:],
+                lhsT=w_code[:, cols].bitcast(FP8X4),
+                lhsT_scale=w_scale[:, cols],
+                rhs=code_of[g][:].bitcast(FP8X4),
+                rhs_scale=scale_of[g][:],
+                start=True,
+                stop=True,
+            )
 
         def vk(s):
             nt = s % NT
-            kt = work.tile([NP, 512], I32, name="kt")
+            kt = ring.tile([NP, 512], I32, name="kt", tag=slot("kt", 3))
             k_of[s] = kt
             ts(kt[:], z_of[s][:], 1.0 / TWO_PI, bturn[:, nt : nt + 1], ALU.mult, ALU.add)
 
         def vr(s):
-            rt = work.tile([NP, 512], F32, name="rt", bufs=8)
+            rt = ring.tile([NP, 512], F32, name="rt", tag=slot("rt", 8))
             r_of[s] = rt
             stt(rt[:], k_of[s][:], -TWO_PI, z_of[s][:], ALU.mult, ALU.add)
 
         def sine(s):
             nt = s % NT
-            st = work.tile([NP, 512], F32, name="st", bufs=8)
+            st = ring.tile([NP, 512], F32, name="st", tag=slot("st", 8))
             s_of[s] = st
             nc.scalar.activation(out=st[:], in_=r_of[s][:], func=ACT.Sin, bias=beta[:, nt : nt + 1], scale=1.0)
 
         def tr(s):
-            o = ps_o.tile([NP, 512], F32, name="o", tag="o")
+            o = ps_o.tile([NP, 512], F32, name="o", tag=slot("o", 4))
             o_of[s] = o
             for j in range(4):
                 nc.tensor.transpose(o[:, j * NP : (j + 1) * NP], s_of[s][:, j * NP : (j + 1) * NP], ident[:])
@@ -238,7 +244,7 @@ def tile_time2vec_t_kernel(tc, x, W, P, w, p, sine_w, cosine_w, out):
 
         x_transposes(0, 0, True)
         x_transposes(0, 1, True)
-        p_t = ps_o.tile([NP, NP], F32, name="p_t", tag="o")
+        p_t = ps_o.tile([NP, NP], F32, name="p_t", tag=slot("o", 4))
         nc.tensor.transpose(p_t[:], p_f32[:], ident[:])
         x_exit(0, 0, False)
         x_exit(0, 1, False)
@@ -296,13 +302,13 @@ def tile_time2vec_t_kernel(tc, x, W, P, w, p, sine_w, cosine_w, out):
             halves = [i + X_LEAD] if i + X_LEAD < 2 * BLOCKS else []
             if i == -1:
                 halves = [2, 3, 4]
-            for xi in halves:
-                x_transposes(xi // 2, xi % 2, xi < 4)
             if i >= 1:
                 for s in range(GROUP * (i - 1), GROUP * i):
                     tr(s)
             for xi in halves:
-                x_exit(xi // 2, xi % 2, False)
+                x_transposes(xi // 2, xi % 2, xi < 4)
             if i >= 1:
                 for s in range(GROUP * (i - 1), GROUP * i):
                     ex(s, s in EXIT_ON_VECTOR)
+            for xi in halves:
+                x_exit(xi // 2, xi % 2, False)

@@ -311,4 +311,4 @@ def tile_time2vec_t_kernel(tc, x, W, P, w, p, sine_w, cosine_w, out):
                 for s in range(GROUP * (i - 1), GROUP * i):
                     ex(s, s in EXIT_ON_VECTOR)
             for xi in halves:
-                x_exit(xi // 2, xi % 2, False)
+                x_exit(xi // 2, xi % 2, xi >= X_LEAD and xi % 2 == 1)

@@ -19,33 +19,29 @@ NP = 128
 BLOCKS = 8
 NT = 8
 STEPS = BLOCKS * NT
+GROUP = 4
+GROUPS = STEPS // GROUP
 TWO_PI = 2.0 * math.pi
 HALF_PI = 0.5 * math.pi
 TINY = 1.0e-30
-STORE_AFTER = {False: {3: 0, 7: 4}, True: {3: 0, 5: 4, 6: 6, 7: 7}}
-GROUP = 4
-GROUPS = STEPS // GROUP
-X_LEAD = 5
-EXIT_ON_VECTOR = (56, 57, 58, 59, 62)
+LIN_ON_GPSIMD = 4
+LIN_AT = (1, 2, 3, 4)
 
 
 def tile_time2vec_t_kernel(tc, x, W, P, w, p, sine_w, cosine_w, out):
     nc = tc.nc
     with ExitStack() as ctx:
         keep = ctx.enter_context(tc.tile_pool(name="keep", bufs=1))
-        xq = ctx.enter_context(tc.tile_pool(name="xq", bufs=2))
-        outp = ctx.enter_context(tc.tile_pool(name="outp", bufs=3))
+        ring = ctx.enter_context(tc.tile_pool(name="ring", bufs=1))
         ps_z = ctx.enter_context(tc.psum_pool(name="ps_z", bufs=1))
         ps_o = ctx.enter_context(tc.psum_pool(name="ps_o", bufs=1))
-        ring = ctx.enter_context(tc.tile_pool(name="ring", bufs=1))
-        turn = {"z": 0, "o": 0, "kt": 0, "rt": 0, "st": 0}
+        ctx.enter_context(tc.manual_schedule())
+        turn = {}
 
         def slot(kind, size):
-            n = turn[kind]
+            n = turn.get(kind, 0)
             turn[kind] = n + 1
             return "%s%d" % (kind, n % size)
-
-        ctx.enter_context(tc.manual_schedule())
 
         x_v = x.rearrange("(g p j) k -> g p j k", p=NP, j=4)
         out_v = out.rearrange("(g p j) m -> g p j m", p=NP, j=4)
@@ -82,7 +78,6 @@ def tile_time2vec_t_kernel(tc, x, W, P, w, p, sine_w, cosine_w, out):
 
         sc = keep.tile([NP, 32], F32, name="sc")
         trig = keep.tile([NP, 2], F32, name="trig")
-        beta = keep.tile([NP, NT], F32, name="beta")
         bturn = keep.tile([NP, NT], F32, name="bturn")
         p_f32 = keep.tile([NP, NP], F32, name="p_f32")
         sn = trig[:, 0:1]
@@ -114,7 +109,7 @@ def tile_time2vec_t_kernel(tc, x, W, P, w, p, sine_w, cosine_w, out):
             if on_vector:
                 nc.vector.tensor_copy(out=dst, in_=src)
             else:
-                nc.scalar.copy(out=dst, in_=src)
+                nc.gpsimd.tensor_scalar(out=dst, in0=src, scalar1=1.0, scalar2=0.0, op0=ALU.mult, op1=ALU.add)
 
         def w_quant(q):
             cols = slice(q * 256, (q + 1) * 256)
@@ -129,27 +124,25 @@ def tile_time2vec_t_kernel(tc, x, W, P, w, p, sine_w, cosine_w, out):
         code_of = {}
         scale_of = {}
 
-        def x_transposes(g, h, in_o_ring):
+        def x_transposes(xi, in_o_ring):
+            g, h = divmod(xi, 2)
             words = x_sb[g][:].bitcast(F32).rearrange("p j (q u) -> p j q u", u=2)
             if in_o_ring:
                 xt = ps_o.tile([NP, 2, 256], F32, name="xt_o", tag=slot("o", 4))
             else:
                 xt = ps_z.tile([NP, 2, 256], F32, name="xt_z", tag=slot("z", 4))
-            xt_of[(g, h)] = xt
+            xt_of[xi] = xt
             for jj in range(2):
                 for u in range(2):
                     nc.tensor.transpose(xt[:, u, jj * NP : (jj + 1) * NP], words[:, 2 * h + jj, :, u], ident[:])
 
-        def x_exit(g, h, on_vector):
+        def x_exit(xi):
+            g, h = divmod(xi, 2)
             if h == 0:
-                grp = xq.tile([NP, 512, 4], BF16, name="grp", align_bytes=64)
+                grp = ring.tile([NP, 512, 4], BF16, name="grp", tag=slot("grp", 2), align_bytes=64)
                 grp_of[g] = grp
             dst = grp_of[g][:].bitcast(F32)[:, h * 256 : (h + 1) * 256, :]
-            src = xt_of[(g, h)][:].rearrange("p u c -> p c u")
-            if on_vector:
-                nc.vector.tensor_copy(out=dst, in_=src)
-            else:
-                nc.scalar.copy(out=dst, in_=src)
+            nc.scalar.copy(out=dst, in_=xt_of[xi][:].rearrange("p u c -> p c u"))
 
         def x_quant(g):
             code = keep.tile([NP, 512], U32, name="code%d" % g, align_bytes=64)
@@ -163,9 +156,7 @@ def tile_time2vec_t_kernel(tc, x, W, P, w, p, sine_w, cosine_w, out):
             )
 
         z_of = {}
-        k_of = {}
-        r_of = {}
-        s_of = {}
+        u_of = {}
         o_of = {}
         ot_of = {}
 
@@ -184,49 +175,61 @@ def tile_time2vec_t_kernel(tc, x, W, P, w, p, sine_w, cosine_w, out):
                 stop=True,
             )
 
-        def vk(s):
+        def turns(s):
             nt = s % NT
-            kt = ring.tile([NP, 512], I32, name="kt", tag=slot("kt", 3))
-            k_of[s] = kt
-            ts(kt[:], z_of[s][:], 1.0 / TWO_PI, bturn[:, nt : nt + 1], ALU.mult, ALU.add)
+            if s % 2 == 0:
+                ut = ring.tile([NP, 2, 512], F32, name="ut", tag=slot("ut", 6))
+                u_of[s // 2] = ut
+            nc.scalar.activation(
+                out=u_of[s // 2][:, s % 2, :], in_=z_of[s][:], func=ACT.Identity,
+                bias=bturn[:, nt : nt + 1], scale=1.0 / TWO_PI,
+            )
 
-        def vr(s):
-            rt = ring.tile([NP, 512], F32, name="rt", tag=slot("rt", 8))
-            r_of[s] = rt
-            stt(rt[:], k_of[s][:], -TWO_PI, z_of[s][:], ALU.mult, ALU.add)
-
-        def sine(s):
-            nt = s % NT
-            st = ring.tile([NP, 512], F32, name="st", tag=slot("st", 8))
-            s_of[s] = st
-            nc.scalar.activation(out=st[:], in_=r_of[s][:], func=ACT.Sin, bias=beta[:, nt : nt + 1], scale=1.0)
+        def fraction(h):
+            flat = u_of[h][:].rearrange("p a b -> p (a b)")
+            kt = ring.tile([NP, 1024], I32, name="kt", tag=slot("kt", 2))
+            nc.vector.tensor_copy(out=kt[:], in_=flat)
+            nc.vector.tensor_tensor(out=flat, in0=flat, in1=kt[:], op=ALU.subtract)
 
         def tr(s):
             o = ps_o.tile([NP, 512], F32, name="o", tag=slot("o", 4))
             o_of[s] = o
             for j in range(4):
-                nc.tensor.transpose(o[:, j * NP : (j + 1) * NP], s_of[s][:, j * NP : (j + 1) * NP], ident[:])
+                nc.tensor.transpose(
+                    o[:, j * NP : (j + 1) * NP], u_of[s // 2][:, s % 2, j * NP : (j + 1) * NP], ident[:]
+                )
 
-        def ex(s, on_vector):
+        def sine(s, width):
+            if s % width == 0:
+                if width == GROUP:
+                    ot = ring.tile([NP, 4, GROUP * NP], F32, name="ot", tag=slot("ot", 5))
+                else:
+                    ot = ring.tile([NP, 4, width * NP], F32, name="ot_last", tag=slot("ot_last", 2))
+                ot_of[s // width] = ot
+            k = s % width
+            nc.scalar.activation(
+                out=ot_of[s // width][:, :, k * NP : (k + 1) * NP],
+                in_=o_of[s][:].rearrange("p (j n) -> p j n", j=4),
+                func=ACT.Sin,
+                scale=TWO_PI,
+            )
+
+        def amplitude(s, width):
             g, nt = divmod(s, NT)
-            dst = ot_of[g][:, :, 512 + nt * NP : 512 + (nt + 1) * NP]
-            src = o_of[s][:].rearrange("p (j n) -> p j n", j=4)
-            if on_vector:
-                nc.vector.tensor_scalar(out=dst, in0=src, scalar1=col(AMP), scalar2=None, op0=ALU.mult)
-            else:
-                nc.scalar.activation(out=dst, in_=src, func=ACT.Copy, scale=col(AMP))
-            first = STORE_AFTER[g == BLOCKS - 1].get(nt)
-            if first is not None:
-                cols = slice(512 + first * NP, 512 + (nt + 1) * NP)
-                nc.sync.dma_start(out=out_v[g][:, :, cols], in_=ot_of[g][:, :, cols])
+            ot = ot_of[s // width]
+            flat = ot[:].rearrange("p j n -> p (j n)")
+            nc.vector.tensor_scalar(out=flat, in0=flat, scalar1=col(AMP), scalar2=None, op0=ALU.mult)
+            nc.sync.dma_start(out=out_v[g][:, :, 512 + (nt + 1 - width) * NP : 512 + (nt + 1) * NP], in_=ot[:])
 
         def lin(g):
-            ot = outp.tile([NP, 4, 1536], F32, name="ot")
-            ot_of[g] = ot
-            nc.gpsimd.tensor_scalar(
-                out=ot[:, :, 0:512], in0=x_sb[g][:], scalar1=col(W32), scalar2=col(P32), op0=ALU.mult, op1=ALU.add
-            )
-            nc.sync.dma_start(out=out_v[g][:, :, 0:512], in_=ot[:, :, 0:512])
+            lt = ring.tile([NP, 4, 512], F32, name="lt", tag=slot("lt", 4))
+            if g < LIN_ON_GPSIMD:
+                nc.gpsimd.tensor_scalar(
+                    out=lt[:], in0=x_sb[g][:], scalar1=col(W32), scalar2=col(P32), op0=ALU.mult, op1=ALU.add
+                )
+            else:
+                ts(lt[:], x_sb[g][:], col(W32), col(P32), ALU.mult, ALU.add)
+            nc.sync.dma_start(out=out_v[g][:, :, 0:512], in_=lt[:])
 
         stt(col(C_ABS), c_bf[:], -1.0, c_bf[:], ALU.mult, ALU.max)
         stt(col(S_ABS), s_bf[:], -1.0, s_bf[:], ALU.mult, ALU.max)
@@ -242,12 +245,16 @@ def tile_time2vec_t_kernel(tc, x, W, P, w, p, sine_w, cosine_w, out):
         nc.vector.tensor_copy(out=col(W32), in_=w_bf[:])
         nc.vector.tensor_copy(out=col(P32), in_=p_bf[:])
 
-        x_transposes(0, 0, True)
-        x_transposes(0, 1, True)
+        x_transposes(0, True)
+        x_transposes(1, True)
         p_t = ps_o.tile([NP, NP], F32, name="p_t", tag=slot("o", 4))
         nc.tensor.transpose(p_t[:], p_f32[:], ident[:])
-        x_exit(0, 0, False)
-        x_exit(0, 1, False)
+        x_exit(0)
+        x_exit(1)
+        for q in range(1, 4):
+            w_regroup(q, False)
+        for g in range(LIN_ON_GPSIMD):
+            lin(g)
 
         ts(col(T1), sn, col(S32), None, ALU.mult, ALU.bypass)
         ts(col(T2), sn, col(C_ABS), TINY, ALU.mult, ALU.max)
@@ -264,51 +271,52 @@ def tile_time2vec_t_kernel(tc, x, W, P, w, p, sine_w, cosine_w, out):
         ts(col(TH), col(HH), col(TT), col(TH0), ALU.mult, ALU.add)
         ts(col(PHI), col(TH), col(HS), 2.0, ALU.mult, ALU.mult)
         ts(bturn[:], p_t[:, 0:NT], col(PHI), 1.0 / TWO_PI, ALU.add, ALU.mult)
-        ts(beta[:], p_t[:, 0:NT], col(PHI), None, ALU.add, ALU.bypass)
         w_quant(0)
         x_quant(0)
-        for q in range(1, 4):
-            w_regroup(q, False)
         w_quant(1)
+        ts(col(G1), col(W2), 1.0 / 16.0, -0.125, ALU.mult, ALU.add)
+        ts(col(G2), col(G1), col(W2), 0.5, ALU.mult, ALU.add)
+        ts(col(G3), col(G2), col(W2), 1.0, ALU.mult, ALU.add)
+        tt(col(AMP), col(G3), col(DEN))
+        w_quant(2)
+        w_quant(3)
 
-        for i in range(-1, GROUPS + 1):
-            if i % 2 == 1 and (i + 1) // 2 < BLOCKS:
-                lin((i + 1) // 2)
-            steps = [s for s in range(GROUP * i + 3, GROUP * i + 7) if 0 <= s < STEPS]
-            for s in steps:
-                mx(s)
-            for s in steps:
-                vk(s)
-                if s >= 1:
-                    vr(s - 1)
-                if s == 0:
-                    ts(col(G1), col(W2), 1.0 / 16.0, -0.125, ALU.mult, ALU.add)
-                    ts(col(G2), col(G1), col(W2), 0.5, ALU.mult, ALU.add)
-                    ts(col(G3), col(G2), col(W2), 1.0, ALU.mult, ALU.add)
-                    tt(col(AMP), col(G3), col(DEN))
-                if s == 1:
-                    w_quant(2)
-                if s == 2:
-                    w_quant(3)
-            if i == GROUPS - 1:
-                vr(STEPS - 1)
-            if i == 0:
-                x_quant(1)
-            if i >= 1 and i % 2 == 1 and (i + 3) // 2 < BLOCKS:
-                x_quant((i + 3) // 2)
-            if 0 <= i < GROUPS:
-                for s in range(GROUP * i, GROUP * i + GROUP):
-                    sine(s)
-            halves = [i + X_LEAD] if i + X_LEAD < 2 * BLOCKS else []
-            if i == -1:
-                halves = [2, 3, 4]
-            if i >= 1:
-                for s in range(GROUP * (i - 1), GROUP * i):
+        for s in range(GROUP):
+            mx(s)
+        x_transposes(2, True)
+        x_transposes(3, True)
+
+        waiting = [2, 3]
+        next_half = 4
+        next_lin = LIN_ON_GPSIMD
+        for i in range(GROUPS + 1):
+            if i < GROUPS:
+                for s in range(GROUP * i, GROUP * (i + 1)):
+                    turns(s)
+                    if s % 2 == 1:
+                        fraction(s // 2)
+            if i + 1 < GROUPS:
+                for s in range(GROUP * (i + 1), GROUP * (i + 2)):
+                    mx(s)
+            if i < GROUPS:
+                for s in range(GROUP * i, GROUP * (i + 1)):
                     tr(s)
-            for xi in halves:
-                x_transposes(xi // 2, xi % 2, xi < 4)
+            fresh = []
+            if next_half < 2 * BLOCKS:
+                fresh = [next_half]
+                x_transposes(next_half, False)
+                next_half += 1
             if i >= 1:
+                width = 2 if i == GROUPS else GROUP
                 for s in range(GROUP * (i - 1), GROUP * i):
-                    ex(s, s in EXIT_ON_VECTOR)
-            for xi in halves:
-                x_exit(xi // 2, xi % 2, xi >= X_LEAD and xi % 2 == 1)
+                    sine(s, width)
+                    if s % width == width - 1:
+                        amplitude(s, width)
+            for xi in waiting:
+                x_exit(xi)
+                if xi % 2 == 1:
+                    x_quant(xi // 2)
+            waiting = fresh
+            if i in LIN_AT and next_lin < BLOCKS:
+                lin(next_lin)
+                next_lin += 1

@@ -19,29 +19,33 @@ NP = 128
 BLOCKS = 8
 NT = 8
 STEPS = BLOCKS * NT
-GROUP = 4
-GROUPS = STEPS // GROUP
 TWO_PI = 2.0 * math.pi
 HALF_PI = 0.5 * math.pi
 TINY = 1.0e-30
-LIN_ON_GPSIMD = 4
-LIN_AT = (1, 2, 3, 4)
+STORE_AFTER = {False: {3: 0, 7: 4}, True: {3: 0, 5: 4, 6: 6, 7: 7}}
+GROUP = 4
+GROUPS = STEPS // GROUP
+X_LEAD = 5
+EXIT_ON_VECTOR = (60, 61)
 
 
 def tile_time2vec_t_kernel(tc, x, W, P, w, p, sine_w, cosine_w, out):
     nc = tc.nc
     with ExitStack() as ctx:
         keep = ctx.enter_context(tc.tile_pool(name="keep", bufs=1))
-        ring = ctx.enter_context(tc.tile_pool(name="ring", bufs=1))
+        xq = ctx.enter_context(tc.tile_pool(name="xq", bufs=2))
+        outp = ctx.enter_context(tc.tile_pool(name="outp", bufs=3))
         ps_z = ctx.enter_context(tc.psum_pool(name="ps_z", bufs=1))
         ps_o = ctx.enter_context(tc.psum_pool(name="ps_o", bufs=1))
-        ctx.enter_context(tc.manual_schedule())
-        turn = {}
+        ring = ctx.enter_context(tc.tile_pool(name="ring", bufs=1))
+        turn = {"z": 0, "o": 0, "kt": 0, "rt": 0, "st": 0}
 
         def slot(kind, size):
-            n = turn.get(kind, 0)
+            n = turn[kind]
             turn[kind] = n + 1
             return "%s%d" % (kind, n % size)
+
+        ctx.enter_context(tc.manual_schedule())
 
         x_v = x.rearrange("(g p j) k -> g p j k", p=NP, j=4)
         out_v = out.rearrange("(g p j) m -> g p j m", p=NP, j=4)
@@ -78,16 +82,22 @@ def tile_time2vec_t_kernel(tc, x, W, P, w, p, sine_w, cosine_w, out):
 
         sc = keep.tile([NP, 32], F32, name="sc")
         trig = keep.tile([NP, 2], F32, name="trig")
+        beta = keep.tile([NP, NT], F32, name="beta")
         bturn = keep.tile([NP, NT], F32, name="bturn")
         p_f32 = keep.tile([NP, NP], F32, name="p_f32")
         sn = trig[:, 0:1]
         cs = trig[:, 1:2]
 
+        gsc = keep.tile([NP, 32], F32, name="gsc")
+
         def col(i):
             return sc[:, i : i + 1]
 
+        def gcol(i):
+            return gsc[:, i : i + 1]
+
         (C_ABS, S_ABS, HS, S32, DD, RD, QQ, TH0, T1, T2, NUM, DEN, RDEN, TT, W2, W4, A1, A2, HH, TH, PHI,
-         G1, G2, G3, AMP, W32, P32) = range(27)
+         G1, G2, G3, AMP, W32, P32, HS2, TH0S, TTS, PHIC) = range(31)
 
         def ts(o, i, s1, s2, op0, op1):
             nc.vector.tensor_scalar(out=o, in0=i, scalar1=s1, scalar2=s2, op0=op0, op1=op1)
@@ -109,7 +119,7 @@ def tile_time2vec_t_kernel(tc, x, W, P, w, p, sine_w, cosine_w, out):
             if on_vector:
                 nc.vector.tensor_copy(out=dst, in_=src)
             else:
-                nc.gpsimd.tensor_scalar(out=dst, in0=src, scalar1=1.0, scalar2=0.0, op0=ALU.mult, op1=ALU.add)
+                nc.scalar.copy(out=dst, in_=src)
 
         def w_quant(q):
             cols = slice(q * 256, (q + 1) * 256)
@@ -124,25 +134,27 @@ def tile_time2vec_t_kernel(tc, x, W, P, w, p, sine_w, cosine_w, out):
         code_of = {}
         scale_of = {}
 
-        def x_transposes(xi, in_o_ring):
-            g, h = divmod(xi, 2)
+        def x_transposes(g, h, in_o_ring):
             words = x_sb[g][:].bitcast(F32).rearrange("p j (q u) -> p j q u", u=2)
             if in_o_ring:
                 xt = ps_o.tile([NP, 2, 256], F32, name="xt_o", tag=slot("o", 4))
             else:
                 xt = ps_z.tile([NP, 2, 256], F32, name="xt_z", tag=slot("z", 4))
-            xt_of[xi] = xt
+            xt_of[(g, h)] = xt
             for jj in range(2):
                 for u in range(2):
                     nc.tensor.transpose(xt[:, u, jj * NP : (jj + 1) * NP], words[:, 2 * h + jj, :, u], ident[:])
 
-        def x_exit(xi):
-            g, h = divmod(xi, 2)
+        def x_exit(g, h, on_vector):
             if h == 0:
-                grp = ring.tile([NP, 512, 4], BF16, name="grp", tag=slot("grp", 2), align_bytes=64)
+                grp = xq.tile([NP, 512, 4], BF16, name="grp", align_bytes=64)
                 grp_of[g] = grp
             dst = grp_of[g][:].bitcast(F32)[:, h * 256 : (h + 1) * 256, :]
-            nc.scalar.copy(out=dst, in_=xt_of[xi][:].rearrange("p u c -> p c u"))
+            src = xt_of[(g, h)][:].rearrange("p u c -> p c u")
+            if on_vector:
+                nc.vector.tensor_copy(out=dst, in_=src)
+            else:
+                nc.scalar.copy(out=dst, in_=src)
 
         def x_quant(g):
             code = keep.tile([NP, 512], U32, name="code%d" % g, align_bytes=64)
@@ -156,7 +168,9 @@ def tile_time2vec_t_kernel(tc, x, W, P, w, p, sine_w, cosine_w, out):
             )
 
         z_of = {}
-        u_of = {}
+        k_of = {}
+        r_of = {}
+        s_of = {}
         o_of = {}
         ot_of = {}
 
@@ -175,61 +189,49 @@ def tile_time2vec_t_kernel(tc, x, W, P, w, p, sine_w, cosine_w, out):
                 stop=True,
             )
 
-        def turns(s):
+        def vk(s):
             nt = s % NT
-            if s % 2 == 0:
-                ut = ring.tile([NP, 2, 512], F32, name="ut", tag=slot("ut", 6))
-                u_of[s // 2] = ut
-            nc.scalar.activation(
-                out=u_of[s // 2][:, s % 2, :], in_=z_of[s][:], func=ACT.Identity,
-                bias=bturn[:, nt : nt + 1], scale=1.0 / TWO_PI,
-            )
+            kt = ring.tile([NP, 512], I32, name="kt", tag=slot("kt", 3))
+            k_of[s] = kt
+            ts(kt[:], z_of[s][:], 1.0 / TWO_PI, bturn[:, nt : nt + 1], ALU.mult, ALU.add)
 
-        def fraction(h):
-            flat = u_of[h][:].rearrange("p a b -> p (a b)")
-            kt = ring.tile([NP, 1024], I32, name="kt", tag=slot("kt", 2))
-            nc.vector.tensor_copy(out=kt[:], in_=flat)
-            nc.vector.tensor_tensor(out=flat, in0=flat, in1=kt[:], op=ALU.subtract)
+        def vr(s):
+            rt = ring.tile([NP, 512], F32, name="rt", tag=slot("rt", 8))
+            r_of[s] = rt
+            stt(rt[:], k_of[s][:], -TWO_PI, z_of[s][:], ALU.mult, ALU.add)
+
+        def sine(s):
+            nt = s % NT
+            st = ring.tile([NP, 512], F32, name="st", tag=slot("st", 8))
+            s_of[s] = st
+            nc.scalar.activation(out=st[:], in_=r_of[s][:], func=ACT.Sin, bias=beta[:, nt : nt + 1], scale=1.0)
 
         def tr(s):
             o = ps_o.tile([NP, 512], F32, name="o", tag=slot("o", 4))
             o_of[s] = o
             for j in range(4):
-                nc.tensor.transpose(
-                    o[:, j * NP : (j + 1) * NP], u_of[s // 2][:, s % 2, j * NP : (j + 1) * NP], ident[:]
-                )
+                nc.tensor.transpose(o[:, j * NP : (j + 1) * NP], s_of[s][:, j * NP : (j + 1) * NP], ident[:])
 
-        def sine(s, width):
-            if s % width == 0:
-                if width == GROUP:
-                    ot = ring.tile([NP, 4, GROUP * NP], F32, name="ot", tag=slot("ot", 5))
-                else:
-                    ot = ring.tile([NP, 4, width * NP], F32, name="ot_last", tag=slot("ot_last", 2))
-                ot_of[s // width] = ot
-            k = s % width
-            nc.scalar.activation(
-                out=ot_of[s // width][:, :, k * NP : (k + 1) * NP],
-                in_=o_of[s][:].rearrange("p (j n) -> p j n", j=4),
-                func=ACT.Sin,
-                scale=TWO_PI,
-            )
-
-        def amplitude(s, width):
+        def ex(s, on_vector):
             g, nt = divmod(s, NT)
-            ot = ot_of[s // width]
-            flat = ot[:].rearrange("p j n -> p (j n)")
-            nc.vector.tensor_scalar(out=flat, in0=flat, scalar1=col(AMP), scalar2=None, op0=ALU.mult)
-            nc.sync.dma_start(out=out_v[g][:, :, 512 + (nt + 1 - width) * NP : 512 + (nt + 1) * NP], in_=ot[:])
+            dst = ot_of[g][:, :, 512 + nt * NP : 512 + (nt + 1) * NP]
+            src = o_of[s][:].rearrange("p (j n) -> p j n", j=4)
+            if on_vector:
+                nc.vector.tensor_scalar(out=dst, in0=src, scalar1=gcol(AMP), scalar2=None, op0=ALU.mult)
+            else:
+                nc.scalar.activation(out=dst, in_=src, func=ACT.Copy, scale=gcol(AMP))
+            first = STORE_AFTER[g == BLOCKS - 1].get(nt)
+            if first is not None:
+                cols = slice(512 + first * NP, 512 + (nt + 1) * NP)
+                nc.sync.dma_start(out=out_v[g][:, :, cols], in_=ot_of[g][:, :, cols])
 
         def lin(g):
-            lt = ring.tile([NP, 4, 512], F32, name="lt", tag=slot("lt", 4))
-            if g < LIN_ON_GPSIMD:
-                nc.gpsimd.tensor_scalar(
-                    out=lt[:], in0=x_sb[g][:], scalar1=col(W32), scalar2=col(P32), op0=ALU.mult, op1=ALU.add
-                )
-            else:
-                ts(lt[:], x_sb[g][:], col(W32), col(P32), ALU.mult, ALU.add)
-            nc.sync.dma_start(out=out_v[g][:, :, 0:512], in_=lt[:])
+            ot = outp.tile([NP, 4, 1536], F32, name="ot")
+            ot_of[g] = ot
+            nc.gpsimd.tensor_scalar(
+                out=ot[:, :, 0:512], in0=x_sb[g][:], scalar1=gcol(W32), scalar2=gcol(P32), op0=ALU.mult, op1=ALU.add
+            )
+            nc.sync.dma_start(out=out_v[g][:, :, 0:512], in_=ot[:, :, 0:512])
 
         stt(col(C_ABS), c_bf[:], -1.0, c_bf[:], ALU.mult, ALU.max)
         stt(col(S_ABS), s_bf[:], -1.0, s_bf[:], ALU.mult, ALU.max)
@@ -241,20 +243,20 @@ def tile_time2vec_t_kernel(tc, x, W, P, w, p, sine_w, cosine_w, out):
         ts(col(TH0), col(QQ), -HALF_PI, HALF_PI, ALU.mult, ALU.add)
         nc.scalar.activation(out=cs, in_=col(QQ), func=ACT.Sin, scale=HALF_PI)
         nc.scalar.activation(out=sn, in_=col(TH0), func=ACT.Sin)
-        nc.vector.tensor_copy(out=p_f32[:], in_=p_rows[:])
-        nc.vector.tensor_copy(out=col(W32), in_=w_bf[:])
-        nc.vector.tensor_copy(out=col(P32), in_=p_bf[:])
+        nc.gpsimd.tensor_copy(out=p_f32[:], in_=p_rows[:])
+        nc.gpsimd.tensor_copy(out=gcol(W32), in_=w_bf[:])
+        nc.gpsimd.tensor_copy(out=gcol(P32), in_=p_bf[:])
+        ts(col(HS2), col(HS), 1.0 / math.pi, None, ALU.mult, ALU.bypass)
+        tt(col(TH0S), col(TH0), col(HS2))
 
-        x_transposes(0, True)
-        x_transposes(1, True)
+        x_transposes(0, 0, True)
+        x_transposes(0, 1, True)
         p_t = ps_o.tile([NP, NP], F32, name="p_t", tag=slot("o", 4))
         nc.tensor.transpose(p_t[:], p_f32[:], ident[:])
-        x_exit(0)
-        x_exit(1)
-        for q in range(1, 4):
+        x_exit(0, 0, False)
+        x_exit(0, 1, False)
+        for q in range(4):
             w_regroup(q, False)
-        for g in range(LIN_ON_GPSIMD):
-            lin(g)
 
         ts(col(T1), sn, col(S32), None, ALU.mult, ALU.bypass)
         ts(col(T2), sn, col(C_ABS), TINY, ALU.mult, ALU.max)
@@ -263,60 +265,61 @@ def tile_time2vec_t_kernel(tc, x, W, P, w, p, sine_w, cosine_w, out):
         nc.vector.reciprocal(out=col(RDEN), in_=col(DEN))
         tt(col(TT), col(NUM), col(RDEN))
         tt(col(W2), col(TT), col(TT))
-        w_regroup(0, True)
-        ts(col(A1), col(W2), -1.0 / 3.0, 1.0, ALU.mult, ALU.add)
+        tt(col(TTS), col(TT), col(HS2))
         ts(col(A2), col(W2), -1.0 / 7.0, 0.2, ALU.mult, ALU.add)
         tt(col(W4), col(W2), col(W2))
+        ts(col(A1), col(W2), -1.0 / 3.0, 1.0, ALU.mult, ALU.add)
         ts(col(HH), col(A2), col(W4), col(A1), ALU.mult, ALU.add)
-        ts(col(TH), col(HH), col(TT), col(TH0), ALU.mult, ALU.add)
-        ts(col(PHI), col(TH), col(HS), 2.0, ALU.mult, ALU.mult)
-        ts(bturn[:], p_t[:, 0:NT], col(PHI), 1.0 / TWO_PI, ALU.add, ALU.mult)
-        w_quant(0)
+        ts(col(PHIC), col(HH), col(TTS), col(TH0S), ALU.mult, ALU.add)
+        ts(bturn[:], p_t[:, 0:NT], 1.0 / TWO_PI, col(PHIC), ALU.mult, ALU.add)
         x_quant(0)
+        w_quant(0)
+        ts(beta[:], bturn[:], TWO_PI, None, ALU.mult, ALU.bypass)
         w_quant(1)
-        ts(col(G1), col(W2), 1.0 / 16.0, -0.125, ALU.mult, ALU.add)
-        ts(col(G2), col(G1), col(W2), 0.5, ALU.mult, ALU.add)
-        ts(col(G3), col(G2), col(W2), 1.0, ALU.mult, ALU.add)
-        tt(col(AMP), col(G3), col(DEN))
-        w_quant(2)
-        w_quant(3)
 
-        for s in range(GROUP):
-            mx(s)
-        x_transposes(2, True)
-        x_transposes(3, True)
+        def gts(o, i, s1, s2):
+            nc.gpsimd.tensor_scalar(out=o, in0=i, scalar1=s1, scalar2=s2, op0=ALU.mult, op1=ALU.add)
 
-        waiting = [2, 3]
-        next_half = 4
-        next_lin = LIN_ON_GPSIMD
-        for i in range(GROUPS + 1):
-            if i < GROUPS:
-                for s in range(GROUP * i, GROUP * (i + 1)):
-                    turns(s)
-                    if s % 2 == 1:
-                        fraction(s // 2)
-            if i + 1 < GROUPS:
-                for s in range(GROUP * (i + 1), GROUP * (i + 2)):
-                    mx(s)
-            if i < GROUPS:
-                for s in range(GROUP * i, GROUP * (i + 1)):
-                    tr(s)
-            fresh = []
-            if next_half < 2 * BLOCKS:
-                fresh = [next_half]
-                x_transposes(next_half, False)
-                next_half += 1
+        gts(gcol(G1), col(W2), 1.0 / 16.0, -0.125)
+        gts(gcol(G2), gcol(G1), col(W2), 0.5)
+        gts(gcol(G3), gcol(G2), col(W2), 1.0)
+        nc.gpsimd.tensor_tensor(out=gcol(AMP), in0=gcol(G3), in1=col(DEN), op=ALU.mult)
+
+        for i in range(-1, GROUPS + 1):
+            if i % 2 == 1 and (i + 1) // 2 < BLOCKS:
+                lin((i + 1) // 2)
+            steps = [s for s in range(GROUP * i + 3, GROUP * i + 7) if 0 <= s < STEPS]
+            for s in steps:
+                mx(s)
+            for s in steps:
+                vk(s)
+                if s >= 1:
+                    vr(s - 1)
+                if s == 1:
+                    w_quant(2)
+                if s == 2:
+                    w_quant(3)
+            if i == GROUPS - 1:
+                vr(STEPS - 1)
+            if i == 0:
+                x_quant(1)
+            if i >= 1 and i % 2 == 1 and (i + 3) // 2 < BLOCKS:
+                x_quant((i + 3) // 2)
+            if 0 <= i < GROUPS - 1:
+                for s in range(GROUP * i, GROUP * i + GROUP):
+                    sine(s)
+            halves = [i + X_LEAD] if i + X_LEAD < 2 * BLOCKS else []
+            if i == -1:
+                halves = [2, 3, 4]
             if i >= 1:
-                width = 2 if i == GROUPS else GROUP
                 for s in range(GROUP * (i - 1), GROUP * i):
-                    sine(s, width)
-                    if s % width == width - 1:
-                        amplitude(s, width)
-            for xi in waiting:
-                x_exit(xi)
-                if xi % 2 == 1:
-                    x_quant(xi // 2)
-            waiting = fresh
-            if i in LIN_AT and next_lin < BLOCKS:
-                lin(next_lin)
-                next_lin += 1
+                    tr(s)
+            for xi in halves:
+                x_transposes(xi // 2, xi % 2, xi < 4)
+            if i >= 1:
+                for s in range(GROUP * (i - 1), GROUP * i):
+                    if i == GROUPS - 1:
+                        sine(s + GROUP)
+                    ex(s, s in EXIT_ON_VECTOR)
+            for xi in halves:
+                x_exit(xi // 2, xi % 2, False)

@@ -15,311 +15,328 @@ FP8X4 = mybir.dt.float8_e4m3fn_x4
 ALU = mybir.AluOpType
 ACT = mybir.ActivationFunctionType
 
-NP = 128
-BLOCKS = 8
-NT = 8
-STEPS = BLOCKS * NT
+PARTS = 128
+PACK = 4
+K = 512
+N = 1024
+BLOCK_ROWS = PARTS * PACK
+BLOCKS = 4096 // BLOCK_ROWS
+HALVES = 2 * BLOCKS
+HALF_ROWS = BLOCK_ROWS // 2
+COL_TILES = N // PARTS
+STEPS = BLOCKS * COL_TILES
+GROUP = 4
+GROUPS = STEPS // GROUP
+W_QUARTER = N // 4
+
+Z_BANKS = 4
+O_BANKS = 4
+K_SLOTS = 3
+R_SLOTS = 2 * GROUP
+S_SLOTS = 2 * GROUP
+GROUPED_SLOTS = 2
+OUT_SLOTS = 3
+
+MX_AHEAD = 3
+X_LEAD = 5
+HEAD_HALVES = 4
+
+STORE_AFTER = {3: 0, 7: 4}
+STORE_AFTER_LAST_BLOCK = {3: 0, 5: 4, 6: 6, 7: 7}
+LEAVE_ON_VECTOR = (STEPS - 4, STEPS - 3)
+
 TWO_PI = 2.0 * math.pi
 HALF_PI = 0.5 * math.pi
 TINY = 1.0e-30
-STORE_AFTER = {False: {3: 0, 7: 4}, True: {3: 0, 5: 4, 6: 6, 7: 7}}
-GROUP = 4
-GROUPS = STEPS // GROUP
-X_LEAD = 5
-EXIT_ON_VECTOR = (60, 61)
 
 
 def tile_time2vec_t_kernel(tc, x, W, P, w, p, sine_w, cosine_w, out):
     nc = tc.nc
     with ExitStack() as ctx:
         keep = ctx.enter_context(tc.tile_pool(name="keep", bufs=1))
-        xq = ctx.enter_context(tc.tile_pool(name="xq", bufs=2))
-        outp = ctx.enter_context(tc.tile_pool(name="outp", bufs=3))
-        ps_z = ctx.enter_context(tc.psum_pool(name="ps_z", bufs=1))
-        ps_o = ctx.enter_context(tc.psum_pool(name="ps_o", bufs=1))
         ring = ctx.enter_context(tc.tile_pool(name="ring", bufs=1))
-        turn = {"z": 0, "o": 0, "kt": 0, "rt": 0, "st": 0}
-
-        def slot(kind, size):
-            n = turn[kind]
-            turn[kind] = n + 1
-            return "%s%d" % (kind, n % size)
-
+        psum = ctx.enter_context(tc.psum_pool(name="psum", bufs=1))
         ctx.enter_context(tc.manual_schedule())
 
-        x_v = x.rearrange("(g p j) k -> g p j k", p=NP, j=4)
-        out_v = out.rearrange("(g p j) m -> g p j m", p=NP, j=4)
-        w_v = W.rearrange("(p j) n -> p j n", j=4)
+        taken = {}
 
-        c_bf = keep.tile([NP, 1], BF16, name="c_bf")
-        s_bf = keep.tile([NP, 1], BF16, name="s_bf")
-        w_bf = keep.tile([NP, 1], BF16, name="w_bf")
-        p_bf = keep.tile([NP, 1], BF16, name="p_bf")
-        p_rows = keep.tile([NP, NP], BF16, name="p_rows")
-        warm = keep.tile([NP, 1], F32, name="warm")
-        warm2 = keep.tile([NP, 1], F32, name="warm2")
-        nc.vector.memset(warm[:], 0.0)
+        def slot(kind, slots):
+            n = taken.get(kind, 0)
+            taken[kind] = n + 1
+            return "%s%d" % (kind, n % slots)
+
+        x_blocks = x.rearrange("(g p j) k -> g p j k", p=PARTS, j=PACK)
+        out_blocks = out.rearrange("(g p j) m -> g p j m", p=PARTS, j=PACK)
+        w_rows = W.rearrange("(p t) n -> p t n", t=PACK)
+
+        c_bf = keep.tile([PARTS, 1], BF16, name="c_bf")
+        s_bf = keep.tile([PARTS, 1], BF16, name="s_bf")
+        w_bf = keep.tile([PARTS, 1], BF16, name="w_bf")
+        p_bf = keep.tile([PARTS, 1], BF16, name="p_bf")
+        p_rows = keep.tile([PARTS, PARTS], BF16, name="p_rows")
+        zero = keep.tile([PARTS, 1], F32, name="zero")
+        unused = keep.tile([PARTS, 1], F32, name="unused")
+        nc.vector.memset(zero[:], 0.0)
         nc.vector.memset(p_rows[:], 0.0)
 
-        nc.scalar.dma_start(out=c_bf[:], in_=cosine_w.partition_broadcast(NP))
-        nc.scalar.dma_start(out=s_bf[:], in_=sine_w.partition_broadcast(NP))
-        nc.scalar.dma_start(out=p_rows[0:8, :], in_=P.rearrange("(t n) -> t n", n=NP))
-        nc.scalar.dma_start(out=w_bf[:], in_=w.partition_broadcast(NP))
-        nc.scalar.dma_start(out=p_bf[:], in_=p.partition_broadcast(NP))
+        nc.scalar.dma_start(out=c_bf[:], in_=cosine_w.partition_broadcast(PARTS))
+        nc.scalar.dma_start(out=s_bf[:], in_=sine_w.partition_broadcast(PARTS))
+        nc.scalar.dma_start(out=p_rows[0:COL_TILES, :], in_=P.rearrange("(t n) -> t n", n=PARTS))
+        nc.scalar.dma_start(out=w_bf[:], in_=w.partition_broadcast(PARTS))
+        nc.scalar.dma_start(out=p_bf[:], in_=p.partition_broadcast(PARTS))
 
-        x_sb = [keep.tile([NP, 4, 512], BF16, name="x_sb%d" % g) for g in range(BLOCKS)]
-        w_raw = keep.tile([NP, 4, 1024], BF16, name="w_raw")
-        nc.sync.dma_start(out=x_sb[0][:], in_=x_v[0])
-        nc.sync.dma_start(out=w_raw[:, :, 0:512], in_=w_v[:, :, 0:512])
-        nc.sync.dma_start(out=w_raw[:, :, 512:1024], in_=w_v[:, :, 512:1024])
+        x_sb = [keep.tile([PARTS, PACK, K], BF16, name="x_sb%d" % g) for g in range(BLOCKS)]
+        w_raw = keep.tile([PARTS, PACK, N], BF16, name="w_raw")
+        nc.sync.dma_start(out=x_sb[0][:], in_=x_blocks[0])
+        nc.sync.dma_start(out=w_raw[:, :, 0 : N // 2], in_=w_rows[:, :, 0 : N // 2])
+        nc.sync.dma_start(out=w_raw[:, :, N // 2 : N], in_=w_rows[:, :, N // 2 : N])
         for g in range(1, BLOCKS):
-            nc.sync.dma_start(out=x_sb[g][:], in_=x_v[g])
+            nc.sync.dma_start(out=x_sb[g][:], in_=x_blocks[g])
 
-        nc.scalar.activation(out=warm2[:], in_=warm[:], func=ACT.Sin)
+        nc.scalar.activation(out=unused[:], in_=zero[:], func=ACT.Sin)
 
-        ident = keep.tile([NP, NP], F32, name="ident")
+        ident = keep.tile([PARTS, PARTS], F32, name="ident")
         make_identity(nc, ident[:])
 
-        sc = keep.tile([NP, 32], F32, name="sc")
-        trig = keep.tile([NP, 2], F32, name="trig")
-        beta = keep.tile([NP, NT], F32, name="beta")
-        bturn = keep.tile([NP, NT], F32, name="bturn")
-        p_f32 = keep.tile([NP, NP], F32, name="p_f32")
-        sn = trig[:, 0:1]
-        cs = trig[:, 1:2]
+        v_names = (
+            "c_abs", "s_abs", "half_sign", "s", "sum", "inv_sum", "q", "theta0", "s_sin", "c_sin", "num", "den",
+            "inv_den", "t", "t2", "t4", "low", "high", "series", "sign_turns", "theta0_turns", "t_turns", "phi_turns",
+        )
+        g_names = ("root1", "root2", "root3", "amplitude", "w", "p")
+        v_tile = keep.tile([PARTS, len(v_names)], F32, name="v_tile")
+        g_tile = keep.tile([PARTS, len(g_names)], F32, name="g_tile")
+        trig = keep.tile([PARTS, 2], F32, name="trig")
+        on_v = {name: v_tile[:, i : i + 1] for i, name in enumerate(v_names)}
+        on_g = {name: g_tile[:, i : i + 1] for i, name in enumerate(g_names)}
+        sin0 = trig[:, 0:1]
+        cos0 = trig[:, 1:2]
+        bias_turns = keep.tile([PARTS, COL_TILES], F32, name="bias_turns")
+        bias = keep.tile([PARTS, COL_TILES], F32, name="bias")
+        p_f32 = keep.tile([PARTS, PARTS], F32, name="p_f32")
 
-        gsc = keep.tile([NP, 32], F32, name="gsc")
-
-        def col(i):
-            return sc[:, i : i + 1]
-
-        def gcol(i):
-            return gsc[:, i : i + 1]
-
-        (C_ABS, S_ABS, HS, S32, DD, RD, QQ, TH0, T1, T2, NUM, DEN, RDEN, TT, W2, W4, A1, A2, HH, TH, PHI,
-         G1, G2, G3, AMP, W32, P32, HS2, TH0S, TTS, PHIC) = range(31)
-
-        def ts(o, i, s1, s2, op0, op1):
+        def v_affine(o, i, s1, s2, op0=ALU.mult, op1=ALU.add):
             nc.vector.tensor_scalar(out=o, in0=i, scalar1=s1, scalar2=s2, op0=op0, op1=op1)
 
-        def stt(o, i0, s, i1, op0, op1):
+        def v_fused(o, i0, s, i1, op0, op1):
             nc.vector.scalar_tensor_tensor(out=o, in0=i0, scalar=s, in1=i1, op0=op0, op1=op1)
 
-        def tt(o, i0, i1):
+        def v_mul(o, i0, i1):
             nc.vector.tensor_tensor(out=o, in0=i0, in1=i1, op=ALU.mult)
 
-        w_grp = keep.tile([NP, 1024, 4], BF16, name="w_grp", align_bytes=64)
-        w_code = keep.tile([NP, 1024], U32, name="w_code", align_bytes=64)
-        w_scale = keep.tile([NP, 1024], U8, name="w_scale", align_bytes=64)
+        def g_affine(o, i, s1, s2):
+            nc.gpsimd.tensor_scalar(out=o, in0=i, scalar1=s1, scalar2=s2, op0=ALU.mult, op1=ALU.add)
 
-        def w_regroup(q, on_vector):
-            cols = slice(q * 256, (q + 1) * 256)
-            dst = w_grp[:, cols, :].rearrange("p (c i) t -> p c t i", i=4)
-            src = w_raw[:, :, cols].rearrange("p t (c i) -> p c t i", i=4)
-            if on_vector:
-                nc.vector.tensor_copy(out=dst, in_=src)
-            else:
-                nc.scalar.copy(out=dst, in_=src)
+        w_grouped = keep.tile([PARTS, N, PACK], BF16, name="w_grouped", align_bytes=64)
+        w_codes = keep.tile([PARTS, N], U32, name="w_codes", align_bytes=64)
+        w_scales = keep.tile([PARTS, N], U8, name="w_scales", align_bytes=64)
 
-        def w_quant(q):
-            cols = slice(q * 256, (q + 1) * 256)
-            nc.vector.quantize_mx(
-                out=w_code[:, cols].bitcast(FP8X4),
-                scales=w_scale[:, cols],
-                in_=w_grp[:, cols, :].rearrange("p c t -> p (c t)"),
+        def regroup_w(q):
+            cols = slice(q * W_QUARTER, (q + 1) * W_QUARTER)
+            nc.scalar.copy(
+                out=w_grouped[:, cols, :].rearrange("p (c i) t -> p c t i", i=4),
+                in_=w_raw[:, :, cols].rearrange("p t (c i) -> p c t i", i=4),
             )
 
-        xt_of = {}
-        grp_of = {}
-        code_of = {}
-        scale_of = {}
+        def quantise_w(q):
+            cols = slice(q * W_QUARTER, (q + 1) * W_QUARTER)
+            nc.vector.quantize_mx(
+                out=w_codes[:, cols].bitcast(FP8X4),
+                scales=w_scales[:, cols],
+                in_=w_grouped[:, cols, :].rearrange("p c t -> p (c t)"),
+            )
 
-        def x_transposes(g, h, in_o_ring):
+        x_t = {}
+        x_grouped = {}
+        x_codes = {}
+        x_scales = {}
+
+        def transpose_x(half):
+            g, h = divmod(half, 2)
             words = x_sb[g][:].bitcast(F32).rearrange("p j (q u) -> p j q u", u=2)
-            if in_o_ring:
-                xt = ps_o.tile([NP, 2, 256], F32, name="xt_o", tag=slot("o", 4))
-            else:
-                xt = ps_z.tile([NP, 2, 256], F32, name="xt_z", tag=slot("z", 4))
-            xt_of[(g, h)] = xt
+            kind, banks = ("o", O_BANKS) if half < HEAD_HALVES else ("z", Z_BANKS)
+            planes = psum.tile([PARTS, 2, HALF_ROWS], F32, name="planes", tag=slot(kind, banks))
+            x_t[half] = planes
             for jj in range(2):
                 for u in range(2):
-                    nc.tensor.transpose(xt[:, u, jj * NP : (jj + 1) * NP], words[:, 2 * h + jj, :, u], ident[:])
+                    nc.tensor.transpose(
+                        planes[:, u, jj * PARTS : (jj + 1) * PARTS], words[:, 2 * h + jj, :, u], ident[:]
+                    )
 
-        def x_exit(g, h, on_vector):
+        def copy_x(half):
+            g, h = divmod(half, 2)
             if h == 0:
-                grp = xq.tile([NP, 512, 4], BF16, name="grp", align_bytes=64)
-                grp_of[g] = grp
-            dst = grp_of[g][:].bitcast(F32)[:, h * 256 : (h + 1) * 256, :]
-            src = xt_of[(g, h)][:].rearrange("p u c -> p c u")
-            if on_vector:
-                nc.vector.tensor_copy(out=dst, in_=src)
-            else:
-                nc.scalar.copy(out=dst, in_=src)
+                grouped = ring.tile(
+                    [PARTS, BLOCK_ROWS, PACK], BF16, name="grouped", tag=slot("grouped", GROUPED_SLOTS), align_bytes=64
+                )
+                x_grouped[g] = grouped
+            nc.scalar.copy(
+                out=x_grouped[g][:].bitcast(F32)[:, h * HALF_ROWS : (h + 1) * HALF_ROWS, :],
+                in_=x_t[half][:].rearrange("p u c -> p c u"),
+            )
 
-        def x_quant(g):
-            code = keep.tile([NP, 512], U32, name="code%d" % g, align_bytes=64)
-            scale = keep.tile([NP, 512], U8, name="scale%d" % g, align_bytes=64)
-            code_of[g] = code
-            scale_of[g] = scale
+        def quantise_x(g):
+            codes = keep.tile([PARTS, BLOCK_ROWS], U32, name="codes%d" % g, align_bytes=64)
+            scales = keep.tile([PARTS, BLOCK_ROWS], U8, name="scales%d" % g, align_bytes=64)
+            x_codes[g] = codes
+            x_scales[g] = scales
             nc.vector.quantize_mx(
-                out=code[:].bitcast(FP8X4),
-                scales=scale[:],
-                in_=grp_of[g][:].rearrange("p c t -> p (c t)"),
+                out=codes[:].bitcast(FP8X4),
+                scales=scales[:],
+                in_=x_grouped[g][:].rearrange("p c t -> p (c t)"),
             )
 
         z_of = {}
         k_of = {}
         r_of = {}
-        s_of = {}
-        o_of = {}
-        ot_of = {}
+        sine_of = {}
+        back_of = {}
+        out_of = {}
 
-        def mx(s):
-            g, nt = divmod(s, NT)
-            z = ps_z.tile([NP, 512], F32, name="z", tag=slot("z", 4))
+        def multiply(s):
+            g, nt = divmod(s, COL_TILES)
+            z = psum.tile([PARTS, BLOCK_ROWS], F32, name="z", tag=slot("z", Z_BANKS))
             z_of[s] = z
-            cols = slice(nt * NP, (nt + 1) * NP)
+            cols = slice(nt * PARTS, (nt + 1) * PARTS)
             nc.tensor.matmul_mx(
                 out=z[:],
-                lhsT=w_code[:, cols].bitcast(FP8X4),
-                lhsT_scale=w_scale[:, cols],
-                rhs=code_of[g][:].bitcast(FP8X4),
-                rhs_scale=scale_of[g][:],
+                lhsT=w_codes[:, cols].bitcast(FP8X4),
+                lhsT_scale=w_scales[:, cols],
+                rhs=x_codes[g][:].bitcast(FP8X4),
+                rhs_scale=x_scales[g][:],
                 start=True,
                 stop=True,
             )
 
-        def vk(s):
-            nt = s % NT
-            kt = ring.tile([NP, 512], I32, name="kt", tag=slot("kt", 3))
-            k_of[s] = kt
-            ts(kt[:], z_of[s][:], 1.0 / TWO_PI, bturn[:, nt : nt + 1], ALU.mult, ALU.add)
+        def round_turns(s):
+            nt = s % COL_TILES
+            k = ring.tile([PARTS, BLOCK_ROWS], I32, name="k", tag=slot("k", K_SLOTS))
+            k_of[s] = k
+            v_affine(k[:], z_of[s][:], 1.0 / TWO_PI, bias_turns[:, nt : nt + 1])
 
-        def vr(s):
-            rt = ring.tile([NP, 512], F32, name="rt", tag=slot("rt", 8))
-            r_of[s] = rt
-            stt(rt[:], k_of[s][:], -TWO_PI, z_of[s][:], ALU.mult, ALU.add)
+        def reduce_argument(s):
+            r = ring.tile([PARTS, BLOCK_ROWS], F32, name="r", tag=slot("r", R_SLOTS))
+            r_of[s] = r
+            v_fused(r[:], k_of[s][:], -TWO_PI, z_of[s][:], ALU.mult, ALU.add)
 
         def sine(s):
-            nt = s % NT
-            st = ring.tile([NP, 512], F32, name="st", tag=slot("st", 8))
-            s_of[s] = st
-            nc.scalar.activation(out=st[:], in_=r_of[s][:], func=ACT.Sin, bias=beta[:, nt : nt + 1], scale=1.0)
+            nt = s % COL_TILES
+            sines = ring.tile([PARTS, BLOCK_ROWS], F32, name="sines", tag=slot("sines", S_SLOTS))
+            sine_of[s] = sines
+            nc.scalar.activation(out=sines[:], in_=r_of[s][:], func=ACT.Sin, bias=bias[:, nt : nt + 1], scale=1.0)
 
-        def tr(s):
-            o = ps_o.tile([NP, 512], F32, name="o", tag=slot("o", 4))
-            o_of[s] = o
-            for j in range(4):
-                nc.tensor.transpose(o[:, j * NP : (j + 1) * NP], s_of[s][:, j * NP : (j + 1) * NP], ident[:])
+        def transpose_back(s):
+            back = psum.tile([PARTS, BLOCK_ROWS], F32, name="back", tag=slot("o", O_BANKS))
+            back_of[s] = back
+            for j in range(PACK):
+                cols = slice(j * PARTS, (j + 1) * PARTS)
+                nc.tensor.transpose(back[:, cols], sine_of[s][:, cols], ident[:])
 
-        def ex(s, on_vector):
-            g, nt = divmod(s, NT)
-            dst = ot_of[g][:, :, 512 + nt * NP : 512 + (nt + 1) * NP]
-            src = o_of[s][:].rearrange("p (j n) -> p j n", j=4)
-            if on_vector:
-                nc.vector.tensor_scalar(out=dst, in0=src, scalar1=gcol(AMP), scalar2=None, op0=ALU.mult)
+        def store(g, first, after):
+            cols = slice(first, after)
+            nc.sync.dma_start(out=out_blocks[g][:, :, cols], in_=out_of[g][:, :, cols])
+
+        def leave_psum(s):
+            g, nt = divmod(s, COL_TILES)
+            dst = out_of[g][:, :, K + nt * PARTS : K + (nt + 1) * PARTS]
+            src = back_of[s][:].rearrange("p (j n) -> p j n", j=PACK)
+            if s in LEAVE_ON_VECTOR:
+                nc.vector.tensor_scalar(out=dst, in0=src, scalar1=on_g["amplitude"], scalar2=None, op0=ALU.mult)
             else:
-                nc.scalar.activation(out=dst, in_=src, func=ACT.Copy, scale=gcol(AMP))
-            first = STORE_AFTER[g == BLOCKS - 1].get(nt)
+                nc.scalar.activation(out=dst, in_=src, func=ACT.Copy, scale=on_g["amplitude"])
+            first = (STORE_AFTER_LAST_BLOCK if g == BLOCKS - 1 else STORE_AFTER).get(nt)
             if first is not None:
-                cols = slice(512 + first * NP, 512 + (nt + 1) * NP)
-                nc.sync.dma_start(out=out_v[g][:, :, cols], in_=ot_of[g][:, :, cols])
+                store(g, K + first * PARTS, K + (nt + 1) * PARTS)
 
-        def lin(g):
-            ot = outp.tile([NP, 4, 1536], F32, name="ot")
-            ot_of[g] = ot
-            nc.gpsimd.tensor_scalar(
-                out=ot[:, :, 0:512], in0=x_sb[g][:], scalar1=gcol(W32), scalar2=gcol(P32), op0=ALU.mult, op1=ALU.add
-            )
-            nc.sync.dma_start(out=out_v[g][:, :, 0:512], in_=ot[:, :, 0:512])
+        def linear_term(g):
+            tile_out = ring.tile([PARTS, PACK, K + N], F32, name="tile_out", tag=slot("out", OUT_SLOTS))
+            out_of[g] = tile_out
+            g_affine(tile_out[:, :, 0:K], x_sb[g][:], on_g["w"], on_g["p"])
+            store(g, 0, K)
 
-        stt(col(C_ABS), c_bf[:], -1.0, c_bf[:], ALU.mult, ALU.max)
-        stt(col(S_ABS), s_bf[:], -1.0, s_bf[:], ALU.mult, ALU.max)
-        nc.vector.tensor_copy(out=col(S32), in_=s_bf[:])
-        stt(col(DD), col(S_ABS), TINY, col(C_ABS), ALU.max, ALU.add)
-        ts(col(HS), c_bf[:], 0.0, 0.5, ALU.is_ge, ALU.subtract)
-        nc.vector.reciprocal(out=col(RD), in_=col(DD))
-        tt(col(QQ), col(S32), col(RD))
-        ts(col(TH0), col(QQ), -HALF_PI, HALF_PI, ALU.mult, ALU.add)
-        nc.scalar.activation(out=cs, in_=col(QQ), func=ACT.Sin, scale=HALF_PI)
-        nc.scalar.activation(out=sn, in_=col(TH0), func=ACT.Sin)
+        v_fused(on_v["c_abs"], c_bf[:], -1.0, c_bf[:], ALU.mult, ALU.max)
+        v_fused(on_v["s_abs"], s_bf[:], -1.0, s_bf[:], ALU.mult, ALU.max)
+        nc.vector.tensor_copy(out=on_v["s"], in_=s_bf[:])
+        v_fused(on_v["sum"], on_v["s_abs"], TINY, on_v["c_abs"], ALU.max, ALU.add)
+        v_affine(on_v["half_sign"], c_bf[:], 0.0, 0.5, ALU.is_ge, ALU.subtract)
+        nc.vector.reciprocal(out=on_v["inv_sum"], in_=on_v["sum"])
+        v_mul(on_v["q"], on_v["s"], on_v["inv_sum"])
+        v_affine(on_v["theta0"], on_v["q"], -HALF_PI, HALF_PI)
+        nc.scalar.activation(out=cos0, in_=on_v["q"], func=ACT.Sin, scale=HALF_PI)
+        nc.scalar.activation(out=sin0, in_=on_v["theta0"], func=ACT.Sin)
         nc.gpsimd.tensor_copy(out=p_f32[:], in_=p_rows[:])
-        nc.gpsimd.tensor_copy(out=gcol(W32), in_=w_bf[:])
-        nc.gpsimd.tensor_copy(out=gcol(P32), in_=p_bf[:])
-        ts(col(HS2), col(HS), 1.0 / math.pi, None, ALU.mult, ALU.bypass)
-        tt(col(TH0S), col(TH0), col(HS2))
+        nc.gpsimd.tensor_copy(out=on_g["w"], in_=w_bf[:])
+        nc.gpsimd.tensor_copy(out=on_g["p"], in_=p_bf[:])
+        v_affine(on_v["sign_turns"], on_v["half_sign"], 1.0 / math.pi, None, ALU.mult, ALU.bypass)
+        v_mul(on_v["theta0_turns"], on_v["theta0"], on_v["sign_turns"])
 
-        x_transposes(0, 0, True)
-        x_transposes(0, 1, True)
-        p_t = ps_o.tile([NP, NP], F32, name="p_t", tag=slot("o", 4))
+        transpose_x(0)
+        transpose_x(1)
+        p_t = psum.tile([PARTS, PARTS], F32, name="p_t", tag=slot("o", O_BANKS))
         nc.tensor.transpose(p_t[:], p_f32[:], ident[:])
-        x_exit(0, 0, False)
-        x_exit(0, 1, False)
+        copy_x(0)
+        copy_x(1)
         for q in range(4):
-            w_regroup(q, False)
+            regroup_w(q)
 
-        ts(col(T1), sn, col(S32), None, ALU.mult, ALU.bypass)
-        ts(col(T2), sn, col(C_ABS), TINY, ALU.mult, ALU.max)
-        stt(col(NUM), cs, col(C_ABS), col(T1), ALU.mult, ALU.subtract)
-        stt(col(DEN), cs, col(S32), col(T2), ALU.mult, ALU.add)
-        nc.vector.reciprocal(out=col(RDEN), in_=col(DEN))
-        tt(col(TT), col(NUM), col(RDEN))
-        tt(col(W2), col(TT), col(TT))
-        tt(col(TTS), col(TT), col(HS2))
-        ts(col(A2), col(W2), -1.0 / 7.0, 0.2, ALU.mult, ALU.add)
-        tt(col(W4), col(W2), col(W2))
-        ts(col(A1), col(W2), -1.0 / 3.0, 1.0, ALU.mult, ALU.add)
-        ts(col(HH), col(A2), col(W4), col(A1), ALU.mult, ALU.add)
-        ts(col(PHIC), col(HH), col(TTS), col(TH0S), ALU.mult, ALU.add)
-        ts(bturn[:], p_t[:, 0:NT], 1.0 / TWO_PI, col(PHIC), ALU.mult, ALU.add)
-        x_quant(0)
-        w_quant(0)
-        ts(beta[:], bturn[:], TWO_PI, None, ALU.mult, ALU.bypass)
-        w_quant(1)
+        v_affine(on_v["s_sin"], sin0, on_v["s"], None, ALU.mult, ALU.bypass)
+        v_affine(on_v["c_sin"], sin0, on_v["c_abs"], TINY, ALU.mult, ALU.max)
+        v_fused(on_v["num"], cos0, on_v["c_abs"], on_v["s_sin"], ALU.mult, ALU.subtract)
+        v_fused(on_v["den"], cos0, on_v["s"], on_v["c_sin"], ALU.mult, ALU.add)
+        nc.vector.reciprocal(out=on_v["inv_den"], in_=on_v["den"])
+        v_mul(on_v["t"], on_v["num"], on_v["inv_den"])
+        v_mul(on_v["t2"], on_v["t"], on_v["t"])
+        v_mul(on_v["t_turns"], on_v["t"], on_v["sign_turns"])
+        v_affine(on_v["high"], on_v["t2"], -1.0 / 7.0, 0.2)
+        v_mul(on_v["t4"], on_v["t2"], on_v["t2"])
+        v_affine(on_v["low"], on_v["t2"], -1.0 / 3.0, 1.0)
+        v_affine(on_v["series"], on_v["high"], on_v["t4"], on_v["low"])
+        v_affine(on_v["phi_turns"], on_v["series"], on_v["t_turns"], on_v["theta0_turns"])
+        v_affine(bias_turns[:], p_t[:, 0:COL_TILES], 1.0 / TWO_PI, on_v["phi_turns"])
+        quantise_x(0)
+        quantise_w(0)
+        v_affine(bias[:], bias_turns[:], TWO_PI, None, ALU.mult, ALU.bypass)
+        quantise_w(1)
 
-        def gts(o, i, s1, s2):
-            nc.gpsimd.tensor_scalar(out=o, in0=i, scalar1=s1, scalar2=s2, op0=ALU.mult, op1=ALU.add)
+        g_affine(on_g["root1"], on_v["t2"], 1.0 / 16.0, -0.125)
+        g_affine(on_g["root2"], on_g["root1"], on_v["t2"], 0.5)
+        g_affine(on_g["root3"], on_g["root2"], on_v["t2"], 1.0)
+        nc.gpsimd.tensor_tensor(out=on_g["amplitude"], in0=on_g["root3"], in1=on_v["den"], op=ALU.mult)
 
-        gts(gcol(G1), col(W2), 1.0 / 16.0, -0.125)
-        gts(gcol(G2), gcol(G1), col(W2), 0.5)
-        gts(gcol(G3), gcol(G2), col(W2), 1.0)
-        nc.gpsimd.tensor_tensor(out=gcol(AMP), in0=gcol(G3), in1=col(DEN), op=ALU.mult)
-
+        copied = []
         for i in range(-1, GROUPS + 1):
             if i % 2 == 1 and (i + 1) // 2 < BLOCKS:
-                lin((i + 1) // 2)
-            steps = [s for s in range(GROUP * i + 3, GROUP * i + 7) if 0 <= s < STEPS]
+                linear_term((i + 1) // 2)
+            first = GROUP * i + MX_AHEAD
+            steps = [s for s in range(first, first + GROUP) if 0 <= s < STEPS]
             for s in steps:
-                mx(s)
+                multiply(s)
             for s in steps:
-                vk(s)
+                round_turns(s)
                 if s >= 1:
-                    vr(s - 1)
-                if s == 1:
-                    w_quant(2)
-                if s == 2:
-                    w_quant(3)
+                    reduce_argument(s - 1)
+                if s in (1, 2):
+                    quantise_w(s + 1)
             if i == GROUPS - 1:
-                vr(STEPS - 1)
-            if i == 0:
-                x_quant(1)
-            if i >= 1 and i % 2 == 1 and (i + 3) // 2 < BLOCKS:
-                x_quant((i + 3) // 2)
+                reduce_argument(STEPS - 1)
+            for half in copied:
+                if half % 2 == 1:
+                    quantise_x(half // 2)
+            before = range(GROUP * (i - 1), GROUP * i) if i >= 1 else []
             if 0 <= i < GROUPS - 1:
-                for s in range(GROUP * i, GROUP * i + GROUP):
+                for s in range(GROUP * i, GROUP * (i + 1)):
                     sine(s)
-            halves = [i + X_LEAD] if i + X_LEAD < 2 * BLOCKS else []
             if i == -1:
                 halves = [2, 3, 4]
-            if i >= 1:
-                for s in range(GROUP * (i - 1), GROUP * i):
-                    tr(s)
-            for xi in halves:
-                x_transposes(xi // 2, xi % 2, xi < 4)
-            if i >= 1:
-                for s in range(GROUP * (i - 1), GROUP * i):
-                    if i == GROUPS - 1:
-                        sine(s + GROUP)
-                    ex(s, s in EXIT_ON_VECTOR)
-            for xi in halves:
-                x_exit(xi // 2, xi % 2, False)
+            else:
+                halves = [half for half in [i + X_LEAD] if half < HALVES]
+            for s in before:
+                transpose_back(s)
+            for half in halves:
+                transpose_x(half)
+            for s in before:
+                if i == GROUPS - 1:
+                    sine(s + GROUP)
+                leave_psum(s)
+            for half in halves:
+                copy_x(half)
+            copied = halves

@@ -25,25 +25,32 @@ HALVES = 2 * BLOCKS
 HALF_ROWS = BLOCK_ROWS // 2
 COL_TILES = N // PARTS
 STEPS = BLOCKS * COL_TILES
-GROUP = 4
-GROUPS = STEPS // GROUP
 W_QUARTER = N // 4
 
+GROUP = 2
 Z_BANKS = 4
 O_BANKS = 4
+X_RING = "o"
+T_LAG = 5
+E_LAG = 3
+DUMMY = 0
 K_SLOTS = 3
-R_SLOTS = 2 * GROUP
-S_SLOTS = 2 * GROUP
+R_SLOTS = 8
+S_SLOTS = 10
 GROUPED_SLOTS = 2
 OUT_SLOTS = 3
-
-MX_AHEAD = 3
-X_LEAD = 5
-HEAD_HALVES = 4
-
-STORE_AFTER = {3: 0, 7: 4}
-STORE_AFTER_LAST_BLOCK = {3: 0, 5: 4, 6: 6, 7: 7}
-LEAVE_ON_VECTOR = (STEPS - 4, STEPS - 3)
+LIN_SLOTS = 4
+LIN_PIECES = 4
+X_AT = 10
+HEAD_BLOCKS = 1
+V_EXITS = 3
+V_EVERY = 0
+VE_LAG = 6
+REGROUP = "vvss"
+X_COPY_LAG = 0
+STORE_STEPS = 4
+FINE_BLOCKS = 1
+XCOPY_V = 0
 
 TWO_PI = 2.0 * math.pi
 HALF_PI = 0.5 * math.pi
@@ -76,20 +83,27 @@ def tile_time2vec_t_kernel(tc, x, W, P, w, p, sine_w, cosine_w, out):
         p_rows = keep.tile([PARTS, PARTS], BF16, name="p_rows")
         zero = keep.tile([PARTS, 1], F32, name="zero")
         unused = keep.tile([PARTS, 1], F32, name="unused")
-        nc.vector.memset(zero[:], 0.0)
         nc.vector.memset(p_rows[:], 0.0)
+        nc.vector.memset(zero[:], 0.0)
 
         nc.scalar.dma_start(out=c_bf[:], in_=cosine_w.partition_broadcast(PARTS))
-        nc.scalar.dma_start(out=s_bf[:], in_=sine_w.partition_broadcast(PARTS))
+        nc.sync.dma_start(out=s_bf[:], in_=sine_w.partition_broadcast(PARTS))
         nc.scalar.dma_start(out=p_rows[0:COL_TILES, :], in_=P.rearrange("(t n) -> t n", n=PARTS))
         nc.scalar.dma_start(out=w_bf[:], in_=w.partition_broadcast(PARTS))
         nc.scalar.dma_start(out=p_bf[:], in_=p.partition_broadcast(PARTS))
 
         x_sb = [keep.tile([PARTS, PACK, K], BF16, name="x_sb%d" % g) for g in range(BLOCKS)]
-        w_raw = keep.tile([PARTS, PACK, N], BF16, name="w_raw")
-        nc.sync.dma_start(out=x_sb[0][:], in_=x_blocks[0])
-        nc.sync.dma_start(out=w_raw[:, :, 0 : N // 2], in_=w_rows[:, :, 0 : N // 2])
-        nc.sync.dma_start(out=w_raw[:, :, N // 2 : N], in_=w_rows[:, :, N // 2 : N])
+        w_raw = [keep.tile([PARTS, PACK, W_QUARTER], BF16, name="w_raw%d" % q) for q in range(4)]
+
+        def load_w(q):
+            nc.sync.dma_start(out=w_raw[q][:], in_=w_rows[:, :, q * W_QUARTER : (q + 1) * W_QUARTER])
+
+        nc.sync.dma_start(out=x_sb[0][:, 0:2, :], in_=x_blocks[0][:, 0:2, :])
+        load_w(0)
+        nc.sync.dma_start(out=x_sb[0][:, 2:4, :], in_=x_blocks[0][:, 2:4, :])
+        load_w(1)
+        load_w(2)
+        load_w(3)
         for g in range(1, BLOCKS):
             nc.sync.dma_start(out=x_sb[g][:], in_=x_blocks[g])
 
@@ -126,23 +140,23 @@ def tile_time2vec_t_kernel(tc, x, W, P, w, p, sine_w, cosine_w, out):
         def g_affine(o, i, s1, s2):
             nc.gpsimd.tensor_scalar(out=o, in0=i, scalar1=s1, scalar2=s2, op0=ALU.mult, op1=ALU.add)
 
-        w_grouped = keep.tile([PARTS, N, PACK], BF16, name="w_grouped", align_bytes=64)
-        w_codes = keep.tile([PARTS, N], U32, name="w_codes", align_bytes=64)
-        w_scales = keep.tile([PARTS, N], U8, name="w_scales", align_bytes=64)
+        w_grouped = [keep.tile([PARTS, W_QUARTER, PACK], BF16, name="w_grouped%d" % q, align_bytes=64) for q in range(4)]
+        w_codes = [keep.tile([PARTS, W_QUARTER], U32, name="w_codes%d" % q, align_bytes=64) for q in range(4)]
+        w_scales = [keep.tile([PARTS, W_QUARTER], U8, name="w_scales%d" % q, align_bytes=64) for q in range(4)]
 
-        def regroup_w(q):
-            cols = slice(q * W_QUARTER, (q + 1) * W_QUARTER)
-            nc.scalar.copy(
-                out=w_grouped[:, cols, :].rearrange("p (c i) t -> p c t i", i=4),
-                in_=w_raw[:, :, cols].rearrange("p t (c i) -> p c t i", i=4),
-            )
+        def regroup_w(q, engine):
+            dst = w_grouped[q][:].rearrange("p (c i) t -> p c t i", i=4)
+            src = w_raw[q][:].rearrange("p t (c i) -> p c t i", i=4)
+            if engine == "s":
+                nc.scalar.copy(out=dst, in_=src)
+            elif engine == "v":
+                nc.vector.tensor_copy(out=dst, in_=src)
+            else:
+                nc.gpsimd.tensor_scalar(out=dst, in0=src, scalar1=1.0, scalar2=0.0, op0=ALU.mult, op1=ALU.add)
 
         def quantise_w(q):
-            cols = slice(q * W_QUARTER, (q + 1) * W_QUARTER)
             nc.vector.quantize_mx(
-                out=w_codes[:, cols].bitcast(FP8X4),
-                scales=w_scales[:, cols],
-                in_=w_grouped[:, cols, :].rearrange("p c t -> p (c t)"),
+                out=w_codes[q][:].bitcast(FP8X4), scales=w_scales[q][:], in_=w_grouped[q][:].rearrange("p c t -> p (c t)")
             )
 
         x_t = {}
@@ -153,26 +167,26 @@ def tile_time2vec_t_kernel(tc, x, W, P, w, p, sine_w, cosine_w, out):
         def transpose_x(half):
             g, h = divmod(half, 2)
             words = x_sb[g][:].bitcast(F32).rearrange("p j (q u) -> p j q u", u=2)
-            kind, banks = ("o", O_BANKS) if half < HEAD_HALVES else ("z", Z_BANKS)
-            planes = psum.tile([PARTS, 2, HALF_ROWS], F32, name="planes", tag=slot(kind, banks))
+            banks = {"o": O_BANKS, "z": Z_BANKS, "x": 1}[X_RING]
+            planes = psum.tile([PARTS, 2, HALF_ROWS], F32, name="planes", tag=slot(X_RING, banks))
             x_t[half] = planes
             for jj in range(2):
                 for u in range(2):
-                    nc.tensor.transpose(
-                        planes[:, u, jj * PARTS : (jj + 1) * PARTS], words[:, 2 * h + jj, :, u], ident[:]
-                    )
+                    nc.tensor.transpose(planes[:, u, jj * PARTS : (jj + 1) * PARTS], words[:, 2 * h + jj, :, u], ident[:])
 
-        def copy_x(half):
+        def copy_x(half, engine):
             g, h = divmod(half, 2)
             if h == 0:
                 grouped = ring.tile(
                     [PARTS, BLOCK_ROWS, PACK], BF16, name="grouped", tag=slot("grouped", GROUPED_SLOTS), align_bytes=64
                 )
                 x_grouped[g] = grouped
-            nc.scalar.copy(
-                out=x_grouped[g][:].bitcast(F32)[:, h * HALF_ROWS : (h + 1) * HALF_ROWS, :],
-                in_=x_t[half][:].rearrange("p u c -> p c u"),
-            )
+            dst = x_grouped[g][:].bitcast(F32)[:, h * HALF_ROWS : (h + 1) * HALF_ROWS, :]
+            src = x_t[half][:].rearrange("p u c -> p c u")
+            if engine == "s":
+                nc.scalar.copy(out=dst, in_=src)
+            else:
+                nc.vector.tensor_copy(out=dst, in_=src)
 
         def quantise_x(g):
             codes = keep.tile([PARTS, BLOCK_ROWS], U32, name="codes%d" % g, align_bytes=64)
@@ -180,9 +194,7 @@ def tile_time2vec_t_kernel(tc, x, W, P, w, p, sine_w, cosine_w, out):
             x_codes[g] = codes
             x_scales[g] = scales
             nc.vector.quantize_mx(
-                out=codes[:].bitcast(FP8X4),
-                scales=scales[:],
-                in_=x_grouped[g][:].rearrange("p c t -> p (c t)"),
+                out=codes[:].bitcast(FP8X4), scales=scales[:], in_=x_grouped[g][:].rearrange("p c t -> p (c t)")
             )
 
         z_of = {}
@@ -192,20 +204,24 @@ def tile_time2vec_t_kernel(tc, x, W, P, w, p, sine_w, cosine_w, out):
         back_of = {}
         out_of = {}
 
-        def multiply(s):
+        def pass_mx(dst, s):
             g, nt = divmod(s, COL_TILES)
-            z = psum.tile([PARTS, BLOCK_ROWS], F32, name="z", tag=slot("z", Z_BANKS))
-            z_of[s] = z
-            cols = slice(nt * PARTS, (nt + 1) * PARTS)
+            q, half = divmod(nt, 2)
+            cols = slice(half * PARTS, (half + 1) * PARTS)
             nc.tensor.matmul_mx(
-                out=z[:],
-                lhsT=w_codes[:, cols].bitcast(FP8X4),
-                lhsT_scale=w_scales[:, cols],
+                out=dst,
+                lhsT=w_codes[q][:, cols].bitcast(FP8X4),
+                lhsT_scale=w_scales[q][:, cols],
                 rhs=x_codes[g][:].bitcast(FP8X4),
                 rhs_scale=x_scales[g][:],
                 start=True,
                 stop=True,
             )
+
+        def multiply(s):
+            z = psum.tile([PARTS, BLOCK_ROWS], F32, name="z", tag=slot("z", Z_BANKS))
+            z_of[s] = z
+            pass_mx(z[:], s)
 
         def round_turns(s):
             nt = s % COL_TILES
@@ -224,34 +240,37 @@ def tile_time2vec_t_kernel(tc, x, W, P, w, p, sine_w, cosine_w, out):
             sine_of[s] = sines
             nc.scalar.activation(out=sines[:], in_=r_of[s][:], func=ACT.Sin, bias=bias[:, nt : nt + 1], scale=1.0)
 
-        def transpose_back(s):
+        def transpose_back(s, dummy_of=None):
             back = psum.tile([PARTS, BLOCK_ROWS], F32, name="back", tag=slot("o", O_BANKS))
             back_of[s] = back
+            if dummy_of is not None:
+                pass_mx(back[:], dummy_of)
             for j in range(PACK):
                 cols = slice(j * PARTS, (j + 1) * PARTS)
                 nc.tensor.transpose(back[:, cols], sine_of[s][:, cols], ident[:])
 
-        def store(g, first, after):
-            cols = slice(first, after)
-            nc.sync.dma_start(out=out_blocks[g][:, :, cols], in_=out_of[g][:, :, cols])
-
-        def leave_psum(s):
+        def leave_psum(s, engine):
             g, nt = divmod(s, COL_TILES)
-            dst = out_of[g][:, :, K + nt * PARTS : K + (nt + 1) * PARTS]
+            if nt == 0:
+                tile_out = ring.tile([PARTS, PACK, N], F32, name="tile_out", tag=slot("out", OUT_SLOTS))
+                out_of[g] = tile_out
+            dst = out_of[g][:, :, nt * PARTS : (nt + 1) * PARTS]
             src = back_of[s][:].rearrange("p (j n) -> p j n", j=PACK)
-            if s in LEAVE_ON_VECTOR:
+            if engine == "v":
                 nc.vector.tensor_scalar(out=dst, in0=src, scalar1=on_g["amplitude"], scalar2=None, op0=ALU.mult)
             else:
                 nc.scalar.activation(out=dst, in_=src, func=ACT.Copy, scale=on_g["amplitude"])
-            first = (STORE_AFTER_LAST_BLOCK if g == BLOCKS - 1 else STORE_AFTER).get(nt)
-            if first is not None:
-                store(g, K + first * PARTS, K + (nt + 1) * PARTS)
+            unit = 1 if g >= BLOCKS - FINE_BLOCKS else STORE_STEPS
+            if (nt + 1) % unit == 0:
+                cols = slice((nt + 1 - unit) * PARTS, (nt + 1) * PARTS)
+                nc.sync.dma_start(out=out_blocks[g][:, :, K + cols.start : K + cols.stop], in_=out_of[g][:, :, cols])
 
         def linear_term(g):
-            tile_out = ring.tile([PARTS, PACK, K + N], F32, name="tile_out", tag=slot("out", OUT_SLOTS))
-            out_of[g] = tile_out
-            g_affine(tile_out[:, :, 0:K], x_sb[g][:], on_g["w"], on_g["p"])
-            store(g, 0, K)
+            lin = ring.tile([PARTS, PACK, K], F32, name="lin", tag=slot("lin", LIN_SLOTS))
+            for j in range(LIN_PIECES):
+                a, b = j * PACK // LIN_PIECES, (j + 1) * PACK // LIN_PIECES
+                g_affine(lin[:, a:b, :], x_sb[g][:, a:b, :], on_g["w"], on_g["p"])
+            nc.gpsimd.dma_start(out=out_blocks[g][:, :, 0:K], in_=lin[:])
 
         v_fused(on_v["c_abs"], c_bf[:], -1.0, c_bf[:], ALU.mult, ALU.max)
         v_fused(on_v["s_abs"], s_bf[:], -1.0, s_bf[:], ALU.mult, ALU.max)
@@ -268,16 +287,6 @@ def tile_time2vec_t_kernel(tc, x, W, P, w, p, sine_w, cosine_w, out):
         nc.gpsimd.tensor_copy(out=on_g["p"], in_=p_bf[:])
         v_affine(on_v["sign_turns"], on_v["half_sign"], 1.0 / math.pi, None, ALU.mult, ALU.bypass)
         v_mul(on_v["theta0_turns"], on_v["theta0"], on_v["sign_turns"])
-
-        transpose_x(0)
-        transpose_x(1)
-        p_t = psum.tile([PARTS, PARTS], F32, name="p_t", tag=slot("o", O_BANKS))
-        nc.tensor.transpose(p_t[:], p_f32[:], ident[:])
-        copy_x(0)
-        copy_x(1)
-        for q in range(4):
-            regroup_w(q)
-
         v_affine(on_v["s_sin"], sin0, on_v["s"], None, ALU.mult, ALU.bypass)
         v_affine(on_v["c_sin"], sin0, on_v["c_abs"], TINY, ALU.mult, ALU.max)
         v_fused(on_v["num"], cos0, on_v["c_abs"], on_v["s_sin"], ALU.mult, ALU.subtract)
@@ -291,52 +300,123 @@ def tile_time2vec_t_kernel(tc, x, W, P, w, p, sine_w, cosine_w, out):
         v_affine(on_v["low"], on_v["t2"], -1.0 / 3.0, 1.0)
         v_affine(on_v["series"], on_v["high"], on_v["t4"], on_v["low"])
         v_affine(on_v["phi_turns"], on_v["series"], on_v["t_turns"], on_v["theta0_turns"])
-        v_affine(bias_turns[:], p_t[:, 0:COL_TILES], 1.0 / TWO_PI, on_v["phi_turns"])
-        quantise_x(0)
-        quantise_w(0)
-        v_affine(bias[:], bias_turns[:], TWO_PI, None, ALU.mult, ALU.bypass)
-        quantise_w(1)
-
         g_affine(on_g["root1"], on_v["t2"], 1.0 / 16.0, -0.125)
         g_affine(on_g["root2"], on_g["root1"], on_v["t2"], 0.5)
         g_affine(on_g["root3"], on_g["root2"], on_v["t2"], 1.0)
         nc.gpsimd.tensor_tensor(out=on_g["amplitude"], in0=on_g["root3"], in1=on_v["den"], op=ALU.mult)
 
-        copied = []
-        for i in range(-1, GROUPS + 1):
-            if i % 2 == 1 and (i + 1) // 2 < BLOCKS:
-                linear_term((i + 1) // 2)
-            first = GROUP * i + MX_AHEAD
-            steps = [s for s in range(first, first + GROUP) if 0 <= s < STEPS]
-            for s in steps:
-                multiply(s)
-            for s in steps:
-                round_turns(s)
-                if s >= 1:
-                    reduce_argument(s - 1)
-                if s in (1, 2):
-                    quantise_w(s + 1)
-            if i == GROUPS - 1:
-                reduce_argument(STEPS - 1)
-            for half in copied:
-                if half % 2 == 1:
-                    quantise_x(half // 2)
-            before = range(GROUP * (i - 1), GROUP * i) if i >= 1 else []
-            if 0 <= i < GROUPS - 1:
-                for s in range(GROUP * i, GROUP * (i + 1)):
-                    sine(s)
-            if i == -1:
-                halves = [2, 3, 4]
-            else:
-                halves = [half for half in [i + X_LEAD] if half < HALVES]
-            for s in before:
-                transpose_back(s)
-            for half in halves:
-                transpose_x(half)
-            for s in before:
-                if i == GROUPS - 1:
-                    sine(s + GROUP)
-                leave_psum(s)
-            for half in halves:
-                copy_x(half)
-            copied = halves
+        prog = {"pe": [], "v": [], "s": [], "g": []}
+
+        def op(engine, key, needs, emit):
+            prog[engine].append((key, needs, emit))
+
+        def x_engine(half):
+            return "v" if half >= 2 * HEAD_BLOCKS and XCOPY_V and half % XCOPY_V == 1 else "s"
+
+        def add_xt(half):
+            op("pe", ("xt", half), [], lambda: transpose_x(half))
+
+        def add_xcopy(half):
+            e = x_engine(half)
+            needs = [("xt", half)] + ([("xc", half - 1)] if half % 2 else [])
+            op(e, ("xc", half), needs, lambda: copy_x(half, e))
+
+        def add_xq(g):
+            op("v", ("xq", g), [("xc", 2 * g), ("xc", 2 * g + 1)], lambda: quantise_x(g))
+
+        def add_wq(q):
+            op("v", ("wq", q), [("wr", q)], lambda: quantise_w(q))
+
+        def add_wr(q):
+            e = REGROUP[q]
+            op(e, ("wr", q), [], lambda: regroup_w(q, e))
+
+        p_of = {}
+
+        def transpose_p():
+            p_t = psum.tile([PARTS, PARTS], F32, name="p_t", tag=slot("z", Z_BANKS))
+            p_of[0] = p_t
+            nc.tensor.transpose(p_t[:], p_f32[:], ident[:])
+
+        def make_bias():
+            v_affine(bias_turns[:], p_of[0][:, 0:COL_TILES], 1.0 / TWO_PI, on_v["phi_turns"])
+            v_affine(bias[:], bias_turns[:], TWO_PI, None, ALU.mult, ALU.bypass)
+
+        def x_step(half):
+            return max(0, 4 * half - X_AT)
+
+        for half in range(2 * HEAD_BLOCKS):
+            add_xt(half)
+        op("pe", ("pt", 0), [], transpose_p)
+        for first in range(0, STEPS + T_LAG + GROUP, GROUP):
+            ms = [s for s in range(first, first + GROUP) if s < STEPS]
+            for s in ms:
+                op("pe", ("m", s), [("xq", s // COL_TILES), ("wq", (s % COL_TILES) // 2)], lambda s=s: multiply(s))
+            ts = [s for s in range(first - T_LAG, first - T_LAG + GROUP) if 0 <= s < STEPS]
+            for n, s in enumerate(ts):
+                d = ms[-1] if (ms and n < DUMMY) else None
+                op("pe", ("t", s), [("sin", s)], lambda s=s, d=d: transpose_back(s, d))
+            for half in range(2 * HEAD_BLOCKS, HALVES):
+                if first <= x_step(half) < first + GROUP:
+                    add_xt(half)
+
+        add_wr(0)
+        add_wq(0)
+        add_wr(1)
+        add_xq(0)
+        add_wq(1)
+        op("v", ("bias", 0), [("pt", 0)], make_bias)
+        wq_at = {1: 2, 2: 3}
+        v_exit = [STEPS - 2 * n - 2 for n in range(V_EXITS)] + [s for s in range(STEPS - 8) if V_EVERY and s % V_EVERY == V_EVERY - 1]
+        for s in range(STEPS + VE_LAG + 1):
+            if s < STEPS:
+                op("v", ("k", s), [("m", s), ("bias", 0)], lambda s=s: round_turns(s))
+            if 1 <= s <= STEPS:
+                op("v", ("r", s - 1), [("k", s - 1)], lambda s=s: reduce_argument(s - 1))
+            if s - VE_LAG in v_exit:
+                op("v", ("e", s - VE_LAG), [("t", s - VE_LAG)] + ([("e", s - VE_LAG - 1)] if (s - VE_LAG) % COL_TILES else []), lambda s=s: leave_psum(s - VE_LAG, "v"))
+            if s in wq_at:
+                add_wq(wq_at[s])
+            if s == 3:
+                for g in range(1, HEAD_BLOCKS):
+                    add_xq(g)
+            for half in range(2 * HEAD_BLOCKS, HALVES):
+                if s == x_step(half) + 2 and x_engine(half) == "v":
+                    add_xcopy(half)
+                if s == x_step(half) + 4 and half % 2 == 1:
+                    add_xq(half // 2)
+
+        add_xcopy(0)
+        add_xcopy(1)
+        for q in range(4):
+            if REGROUP[q] == "s":
+                add_wr(q)
+        for half in range(2, 2 * HEAD_BLOCKS):
+            add_xcopy(half)
+        for s in range(STEPS + E_LAG):
+            if s < STEPS:
+                op("s", ("sin", s), [("r", s)], lambda s=s: sine(s))
+            e = s - E_LAG
+            if e >= 0 and e not in v_exit:
+                op("s", ("e", e), [("t", e)] + ([("e", e - 1)] if e % COL_TILES else []), lambda e=e: leave_psum(e, "s"))
+            for half in range(2 * HEAD_BLOCKS, HALVES):
+                if s == x_step(half) + X_COPY_LAG and x_engine(half) == "s":
+                    add_xcopy(half)
+
+        for q in range(4):
+            if REGROUP[q] == "g":
+                add_wr(q)
+        for g in range(BLOCKS):
+            op("g", ("lin", g), [], lambda g=g: linear_term(g))
+
+        done = set()
+        at = {e: 0 for e in prog}
+        total = sum(len(v) for v in prog.values())
+        for turn in range(total):
+            for e in ("pe", "v", "s", "g"):
+                for n in range(2 * GROUP + 2 if e == "pe" else 1):
+                    if at[e] < len(prog[e]) and all(need in done for need in prog[e][at[e]][1]):
+                        prog[e][at[e]][2]()
+                        done.add(prog[e][at[e]][0])
+                        at[e] += 1
+        assert len(done) == total, "the programs wait for each other"

@@ -34,9 +34,8 @@ X_RING = "o"
 T_LAG = 5
 E_LAG = 3
 DUMMY = 0
-K_SLOTS = 3
-R_SLOTS = 8
-S_SLOTS = 10
+K_SLOTS = 5
+R_SLOTS = 12
 GROUPED_SLOTS = 2
 OUT_SLOTS = 3
 LIN_SLOTS = 4
@@ -48,6 +47,8 @@ V_EVERY = 0
 VE_LAG = 6
 REGROUP = "vvss"
 X_COPY_LAG = 0
+WQ1_FIRST = 1
+WQ_AT = (0, 1, 2)
 STORE_STEPS = 4
 FINE_BLOCKS = 1
 XCOPY_V = 0
@@ -236,15 +237,17 @@ def tile_time2vec_t_kernel(tc, x, W, P, w, p, sine_w, cosine_w, out):
 
         def sine(s):
             nt = s % COL_TILES
-            sines = ring.tile([PARTS, BLOCK_ROWS], F32, name="sines", tag=slot("sines", S_SLOTS))
-            sine_of[s] = sines
-            nc.scalar.activation(out=sines[:], in_=r_of[s][:], func=ACT.Sin, bias=bias[:, nt : nt + 1], scale=1.0)
+            sine_of[s] = r_of[s]
+            nc.scalar.activation(out=r_of[s][:], in_=r_of[s][:], func=ACT.Sin, bias=bias[:, nt : nt + 1], scale=1.0)
 
-        def transpose_back(s, dummy_of=None):
+        def open_back(s, dummy_of=None):
             back = psum.tile([PARTS, BLOCK_ROWS], F32, name="back", tag=slot("o", O_BANKS))
             back_of[s] = back
             if dummy_of is not None:
                 pass_mx(back[:], dummy_of)
+
+        def transpose_back(s):
+            back = back_of[s]
             for j in range(PACK):
                 cols = slice(j * PARTS, (j + 1) * PARTS)
                 nc.tensor.transpose(back[:, cols], sine_of[s][:, cols], ident[:])
@@ -354,19 +357,25 @@ def tile_time2vec_t_kernel(tc, x, W, P, w, p, sine_w, cosine_w, out):
                 op("pe", ("m", s), [("xq", s // COL_TILES), ("wq", (s % COL_TILES) // 2)], lambda s=s: multiply(s))
             ts = [s for s in range(first - T_LAG, first - T_LAG + GROUP) if 0 <= s < STEPS]
             for n, s in enumerate(ts):
-                d = ms[-1] if (ms and n < DUMMY) else None
-                op("pe", ("t", s), [("sin", s)], lambda s=s, d=d: transpose_back(s, d))
+                d = min(first + GROUP - 1, STEPS - 1) if n < DUMMY else None
+                op("pe", ("ob", s), [], lambda s=s, d=d: open_back(s, d))
+            for s in ts:
+                op("pe", ("t", s), [("sin", s)], lambda s=s: transpose_back(s))
             for half in range(2 * HEAD_BLOCKS, HALVES):
                 if first <= x_step(half) < first + GROUP:
                     add_xt(half)
 
         add_wr(0)
         add_wq(0)
-        add_wr(1)
-        add_xq(0)
-        add_wq(1)
+        if WQ1_FIRST:
+            if REGROUP[1] == "v":
+                add_wr(1)
+            add_xq(0)
+            add_wq(1)
+        else:
+            add_xq(0)
         op("v", ("bias", 0), [("pt", 0)], make_bias)
-        wq_at = {1: 2, 2: 3}
+        wq_at = {WQ_AT[n]: n + 1 for n in range(1 if WQ1_FIRST else 0, 3)}
         v_exit = [STEPS - 2 * n - 2 for n in range(V_EXITS)] + [s for s in range(STEPS - 8) if V_EVERY and s % V_EVERY == V_EVERY - 1]
         for s in range(STEPS + VE_LAG + 1):
             if s < STEPS:
@@ -376,6 +385,8 @@ def tile_time2vec_t_kernel(tc, x, W, P, w, p, sine_w, cosine_w, out):
             if s - VE_LAG in v_exit:
                 op("v", ("e", s - VE_LAG), [("t", s - VE_LAG)] + ([("e", s - VE_LAG - 1)] if (s - VE_LAG) % COL_TILES else []), lambda s=s: leave_psum(s - VE_LAG, "v"))
             if s in wq_at:
+                if REGROUP[wq_at[s]] == "v":
+                    add_wr(wq_at[s])
                 add_wq(wq_at[s])
             if s == 3:
                 for g in range(1, HEAD_BLOCKS):
@@ -414,7 +425,7 @@ def tile_time2vec_t_kernel(tc, x, W, P, w, p, sine_w, cosine_w, out):
         total = sum(len(v) for v in prog.values())
         for turn in range(total):
             for e in ("pe", "v", "s", "g"):
-                for n in range(2 * GROUP + 2 if e == "pe" else 1):
+                for n in range(3 * GROUP + 2 if e == "pe" else 1):
                     if at[e] < len(prog[e]) and all(need in done for need in prog[e][at[e]][1]):
                         prog[e][at[e]][2]()
                         done.add(prog[e][at[e]][0])

@@ -45,13 +45,19 @@ HEAD_BLOCKS = 1
 V_EXITS = 3
 V_EVERY = 0
 VE_LAG = 6
-REGROUP = "vvss"
+W_PIECES = ((0, 128, "v"), (128, 256, "v"), (256, 512, "s"), (512, 768, "s"), (768, 1024, "s"))
 X_COPY_LAG = 0
-WQ1_FIRST = 1
-WQ_AT = (0, 1, 2)
+XQ_LAG = 4
+WARM = 0
+WQ_AT = {0: 2, 1: 3, 2: 4}
 STORE_STEPS = 4
 FINE_BLOCKS = 1
 XCOPY_V = 0
+
+V_HEAD = (
+    "c_abs s_abs s half_sign sum inv_sum q sign_turns wr0 theta0 s_sin c_sin num den wq0 inv_den wr1 t xq0a t2 t_turns "
+    "theta0_turns high t4 low series xq0b phi_turns bias_turns wq1"
+)
 
 TWO_PI = 2.0 * math.pi
 HALF_PI = 0.5 * math.pi
@@ -85,19 +91,21 @@ def tile_time2vec_t_kernel(tc, x, W, P, w, p, sine_w, cosine_w, out):
         zero = keep.tile([PARTS, 1], F32, name="zero")
         unused = keep.tile([PARTS, 1], F32, name="unused")
         nc.vector.memset(p_rows[:], 0.0)
+        if WARM:
+            idle = keep.tile([PARTS, BLOCK_ROWS], BF16, name="idle")
+            nc.vector.memset(idle[:], 0.0)
         nc.vector.memset(zero[:], 0.0)
 
         nc.scalar.dma_start(out=c_bf[:], in_=cosine_w.partition_broadcast(PARTS))
         nc.sync.dma_start(out=s_bf[:], in_=sine_w.partition_broadcast(PARTS))
         nc.scalar.dma_start(out=p_rows[0:COL_TILES, :], in_=P.rearrange("(t n) -> t n", n=PARTS))
-        nc.scalar.dma_start(out=w_bf[:], in_=w.partition_broadcast(PARTS))
-        nc.scalar.dma_start(out=p_bf[:], in_=p.partition_broadcast(PARTS))
 
         x_sb = [keep.tile([PARTS, PACK, K], BF16, name="x_sb%d" % g) for g in range(BLOCKS)]
-        w_raw = [keep.tile([PARTS, PACK, W_QUARTER], BF16, name="w_raw%d" % q) for q in range(4)]
+        w_raw = keep.tile([PARTS, PACK, N], BF16, name="w_raw")
 
         def load_w(q):
-            nc.sync.dma_start(out=w_raw[q][:], in_=w_rows[:, :, q * W_QUARTER : (q + 1) * W_QUARTER])
+            cols = slice(q * W_QUARTER, (q + 1) * W_QUARTER)
+            nc.sync.dma_start(out=w_raw[:, :, cols], in_=w_rows[:, :, cols])
 
         nc.sync.dma_start(out=x_sb[0][:, 0:2, :], in_=x_blocks[0][:, 0:2, :])
         load_w(0)
@@ -107,6 +115,9 @@ def tile_time2vec_t_kernel(tc, x, W, P, w, p, sine_w, cosine_w, out):
         load_w(3)
         for g in range(1, BLOCKS):
             nc.sync.dma_start(out=x_sb[g][:], in_=x_blocks[g])
+            if g == 1:
+                nc.sync.dma_start(out=w_bf[:], in_=w.partition_broadcast(PARTS))
+                nc.sync.dma_start(out=p_bf[:], in_=p.partition_broadcast(PARTS))
 
         nc.scalar.activation(out=unused[:], in_=zero[:], func=ACT.Sin)
 
@@ -141,23 +152,25 @@ def tile_time2vec_t_kernel(tc, x, W, P, w, p, sine_w, cosine_w, out):
         def g_affine(o, i, s1, s2):
             nc.gpsimd.tensor_scalar(out=o, in0=i, scalar1=s1, scalar2=s2, op0=ALU.mult, op1=ALU.add)
 
-        w_grouped = [keep.tile([PARTS, W_QUARTER, PACK], BF16, name="w_grouped%d" % q, align_bytes=64) for q in range(4)]
-        w_codes = [keep.tile([PARTS, W_QUARTER], U32, name="w_codes%d" % q, align_bytes=64) for q in range(4)]
-        w_scales = [keep.tile([PARTS, W_QUARTER], U8, name="w_scales%d" % q, align_bytes=64) for q in range(4)]
+        w_grouped = keep.tile([PARTS, N, PACK], BF16, name="w_grouped", align_bytes=64)
+        w_codes = keep.tile([PARTS, N], U32, name="w_codes", align_bytes=64)
+        w_scales = keep.tile([PARTS, N], U8, name="w_scales", align_bytes=64)
 
-        def regroup_w(q, engine):
-            dst = w_grouped[q][:].rearrange("p (c i) t -> p c t i", i=4)
-            src = w_raw[q][:].rearrange("p t (c i) -> p c t i", i=4)
+        def regroup_w(piece):
+            first, after, engine = W_PIECES[piece]
+            dst = w_grouped[:, first:after, :].rearrange("p (c i) t -> p c t i", i=4)
+            src = w_raw[:, :, first:after].rearrange("p t (c i) -> p c t i", i=4)
             if engine == "s":
                 nc.scalar.copy(out=dst, in_=src)
-            elif engine == "v":
-                nc.vector.tensor_copy(out=dst, in_=src)
             else:
-                nc.gpsimd.tensor_scalar(out=dst, in0=src, scalar1=1.0, scalar2=0.0, op0=ALU.mult, op1=ALU.add)
+                nc.vector.tensor_copy(out=dst, in_=src)
 
-        def quantise_w(q):
+        def quantise_w(piece):
+            first, after, engine = W_PIECES[piece]
             nc.vector.quantize_mx(
-                out=w_codes[q][:].bitcast(FP8X4), scales=w_scales[q][:], in_=w_grouped[q][:].rearrange("p c t -> p (c t)")
+                out=w_codes[:, first:after].bitcast(FP8X4),
+                scales=w_scales[:, first:after],
+                in_=w_grouped[:, first:after, :].rearrange("p c t -> p (c t)"),
             )
 
         x_t = {}
@@ -189,13 +202,16 @@ def tile_time2vec_t_kernel(tc, x, W, P, w, p, sine_w, cosine_w, out):
             else:
                 nc.vector.tensor_copy(out=dst, in_=src)
 
-        def quantise_x(g):
-            codes = keep.tile([PARTS, BLOCK_ROWS], U32, name="codes%d" % g, align_bytes=64)
-            scales = keep.tile([PARTS, BLOCK_ROWS], U8, name="scales%d" % g, align_bytes=64)
-            x_codes[g] = codes
-            x_scales[g] = scales
+        def quantise_x(g, first=0, after=BLOCK_ROWS):
+            if first == 0:
+                codes = keep.tile([PARTS, BLOCK_ROWS], U32, name="codes%d" % g, align_bytes=64)
+                scales = keep.tile([PARTS, BLOCK_ROWS], U8, name="scales%d" % g, align_bytes=64)
+                x_codes[g] = codes
+                x_scales[g] = scales
             nc.vector.quantize_mx(
-                out=codes[:].bitcast(FP8X4), scales=scales[:], in_=x_grouped[g][:].rearrange("p c t -> p (c t)")
+                out=x_codes[g][:, first:after].bitcast(FP8X4),
+                scales=x_scales[g][:, first:after],
+                in_=x_grouped[g][:, first:after, :].rearrange("p c t -> p (c t)"),
             )
 
         z_of = {}
@@ -207,12 +223,11 @@ def tile_time2vec_t_kernel(tc, x, W, P, w, p, sine_w, cosine_w, out):
 
         def pass_mx(dst, s):
             g, nt = divmod(s, COL_TILES)
-            q, half = divmod(nt, 2)
-            cols = slice(half * PARTS, (half + 1) * PARTS)
+            cols = slice(nt * PARTS, (nt + 1) * PARTS)
             nc.tensor.matmul_mx(
                 out=dst,
-                lhsT=w_codes[q][:, cols].bitcast(FP8X4),
-                lhsT_scale=w_scales[q][:, cols],
+                lhsT=w_codes[:, cols].bitcast(FP8X4),
+                lhsT_scale=w_scales[:, cols],
                 rhs=x_codes[g][:].bitcast(FP8X4),
                 rhs_scale=x_scales[g][:],
                 start=True,
@@ -275,38 +290,46 @@ def tile_time2vec_t_kernel(tc, x, W, P, w, p, sine_w, cosine_w, out):
                 g_affine(lin[:, a:b, :], x_sb[g][:, a:b, :], on_g["w"], on_g["p"])
             nc.gpsimd.dma_start(out=out_blocks[g][:, :, 0:K], in_=lin[:])
 
-        v_fused(on_v["c_abs"], c_bf[:], -1.0, c_bf[:], ALU.mult, ALU.max)
-        v_fused(on_v["s_abs"], s_bf[:], -1.0, s_bf[:], ALU.mult, ALU.max)
-        nc.vector.tensor_copy(out=on_v["s"], in_=s_bf[:])
-        v_fused(on_v["sum"], on_v["s_abs"], TINY, on_v["c_abs"], ALU.max, ALU.add)
-        v_affine(on_v["half_sign"], c_bf[:], 0.0, 0.5, ALU.is_ge, ALU.subtract)
-        nc.vector.reciprocal(out=on_v["inv_sum"], in_=on_v["sum"])
-        v_mul(on_v["q"], on_v["s"], on_v["inv_sum"])
-        v_affine(on_v["theta0"], on_v["q"], -HALF_PI, HALF_PI)
-        nc.scalar.activation(out=cos0, in_=on_v["q"], func=ACT.Sin, scale=HALF_PI)
-        nc.scalar.activation(out=sin0, in_=on_v["theta0"], func=ACT.Sin)
-        nc.gpsimd.tensor_copy(out=p_f32[:], in_=p_rows[:])
-        nc.gpsimd.tensor_copy(out=on_g["w"], in_=w_bf[:])
-        nc.gpsimd.tensor_copy(out=on_g["p"], in_=p_bf[:])
-        v_affine(on_v["sign_turns"], on_v["half_sign"], 1.0 / math.pi, None, ALU.mult, ALU.bypass)
-        v_mul(on_v["theta0_turns"], on_v["theta0"], on_v["sign_turns"])
-        v_affine(on_v["s_sin"], sin0, on_v["s"], None, ALU.mult, ALU.bypass)
-        v_affine(on_v["c_sin"], sin0, on_v["c_abs"], TINY, ALU.mult, ALU.max)
-        v_fused(on_v["num"], cos0, on_v["c_abs"], on_v["s_sin"], ALU.mult, ALU.subtract)
-        v_fused(on_v["den"], cos0, on_v["s"], on_v["c_sin"], ALU.mult, ALU.add)
-        nc.vector.reciprocal(out=on_v["inv_den"], in_=on_v["den"])
-        v_mul(on_v["t"], on_v["num"], on_v["inv_den"])
-        v_mul(on_v["t2"], on_v["t"], on_v["t"])
-        v_mul(on_v["t_turns"], on_v["t"], on_v["sign_turns"])
-        v_affine(on_v["high"], on_v["t2"], -1.0 / 7.0, 0.2)
-        v_mul(on_v["t4"], on_v["t2"], on_v["t2"])
-        v_affine(on_v["low"], on_v["t2"], -1.0 / 3.0, 1.0)
-        v_affine(on_v["series"], on_v["high"], on_v["t4"], on_v["low"])
-        v_affine(on_v["phi_turns"], on_v["series"], on_v["t_turns"], on_v["theta0_turns"])
-        g_affine(on_g["root1"], on_v["t2"], 1.0 / 16.0, -0.125)
-        g_affine(on_g["root2"], on_g["root1"], on_v["t2"], 0.5)
-        g_affine(on_g["root3"], on_g["root2"], on_v["t2"], 1.0)
-        nc.gpsimd.tensor_tensor(out=on_g["amplitude"], in0=on_g["root3"], in1=on_v["den"], op=ALU.mult)
+        chain = {
+            "c_abs": lambda: v_fused(on_v["c_abs"], c_bf[:], -1.0, c_bf[:], ALU.mult, ALU.max),
+            "s_abs": lambda: v_fused(on_v["s_abs"], s_bf[:], -1.0, s_bf[:], ALU.mult, ALU.max),
+            "s": lambda: nc.vector.tensor_copy(out=on_v["s"], in_=s_bf[:]),
+            "half_sign": lambda: v_affine(on_v["half_sign"], c_bf[:], 0.0, 0.5, ALU.is_ge, ALU.subtract),
+            "sum": lambda: v_fused(on_v["sum"], on_v["s_abs"], TINY, on_v["c_abs"], ALU.max, ALU.add),
+            "inv_sum": lambda: nc.vector.reciprocal(out=on_v["inv_sum"], in_=on_v["sum"]),
+            "q": lambda: v_mul(on_v["q"], on_v["s"], on_v["inv_sum"]),
+            "theta0": lambda: v_affine(on_v["theta0"], on_v["q"], -HALF_PI, HALF_PI),
+            "sign_turns": lambda: v_affine(on_v["sign_turns"], on_v["half_sign"], 1.0 / math.pi, None, ALU.mult, ALU.bypass),
+            "theta0_turns": lambda: v_mul(on_v["theta0_turns"], on_v["theta0"], on_v["sign_turns"]),
+            "s_sin": lambda: v_affine(on_v["s_sin"], sin0, on_v["s"], None, ALU.mult, ALU.bypass),
+            "c_sin": lambda: v_affine(on_v["c_sin"], sin0, on_v["c_abs"], TINY, ALU.mult, ALU.max),
+            "num": lambda: v_fused(on_v["num"], cos0, on_v["c_abs"], on_v["s_sin"], ALU.mult, ALU.subtract),
+            "den": lambda: v_fused(on_v["den"], cos0, on_v["s"], on_v["c_sin"], ALU.mult, ALU.add),
+            "inv_den": lambda: nc.vector.reciprocal(out=on_v["inv_den"], in_=on_v["den"]),
+            "t": lambda: v_mul(on_v["t"], on_v["num"], on_v["inv_den"]),
+            "t2": lambda: v_mul(on_v["t2"], on_v["t"], on_v["t"]),
+            "t_turns": lambda: v_mul(on_v["t_turns"], on_v["t"], on_v["sign_turns"]),
+            "high": lambda: v_affine(on_v["high"], on_v["t2"], -1.0 / 7.0, 0.2),
+            "t4": lambda: v_mul(on_v["t4"], on_v["t2"], on_v["t2"]),
+            "low": lambda: v_affine(on_v["low"], on_v["t2"], -1.0 / 3.0, 1.0),
+            "series": lambda: v_affine(on_v["series"], on_v["high"], on_v["t4"], on_v["low"]),
+            "phi_turns": lambda: v_affine(on_v["phi_turns"], on_v["series"], on_v["t_turns"], on_v["theta0_turns"]),
+        }
+
+        def trig():
+            nc.scalar.activation(out=cos0, in_=on_v["q"], func=ACT.Sin, scale=HALF_PI)
+            nc.scalar.activation(out=sin0, in_=on_v["q"], func=ACT.Sin, scale=-HALF_PI, bias=HALF_PI)
+
+        def casts():
+            nc.gpsimd.tensor_copy(out=p_f32[:], in_=p_rows[:])
+
+        def amplitude():
+            g_affine(on_g["root1"], on_v["t2"], 1.0 / 16.0, -0.125)
+            g_affine(on_g["root2"], on_g["root1"], on_v["t2"], 0.5)
+            g_affine(on_g["root3"], on_g["root2"], on_v["t2"], 1.0)
+            nc.gpsimd.tensor_tensor(out=on_g["amplitude"], in0=on_g["root3"], in1=on_v["den"], op=ALU.mult)
+            nc.gpsimd.tensor_copy(out=on_g["w"], in_=w_bf[:])
+            nc.gpsimd.tensor_copy(out=on_g["p"], in_=p_bf[:])
 
         prog = {"pe": [], "v": [], "s": [], "g": []}
 
@@ -327,12 +350,14 @@ def tile_time2vec_t_kernel(tc, x, W, P, w, p, sine_w, cosine_w, out):
         def add_xq(g):
             op("v", ("xq", g), [("xc", 2 * g), ("xc", 2 * g + 1)], lambda: quantise_x(g))
 
-        def add_wq(q):
-            op("v", ("wq", q), [("wr", q)], lambda: quantise_w(q))
+        def add_wq(piece):
+            op("v", ("wq", piece), [("wr", piece)], lambda: quantise_w(piece))
 
-        def add_wr(q):
-            e = REGROUP[q]
-            op(e, ("wr", q), [], lambda: regroup_w(q, e))
+        def add_wr(piece):
+            op(W_PIECES[piece][2], ("wr", piece), [], lambda: regroup_w(piece))
+
+        def piece_of(nt):
+            return [n for n, piece in enumerate(W_PIECES) if piece[0] <= nt * PARTS < piece[1]][0]
 
         p_of = {}
 
@@ -341,20 +366,23 @@ def tile_time2vec_t_kernel(tc, x, W, P, w, p, sine_w, cosine_w, out):
             p_of[0] = p_t
             nc.tensor.transpose(p_t[:], p_f32[:], ident[:])
 
-        def make_bias():
-            v_affine(bias_turns[:], p_of[0][:, 0:COL_TILES], 1.0 / TWO_PI, on_v["phi_turns"])
-            v_affine(bias[:], bias_turns[:], TWO_PI, None, ALU.mult, ALU.bypass)
-
         def x_step(half):
             return max(0, 4 * half - X_AT)
 
+        def warm_up():
+            nobody = psum.tile([PARTS, BLOCK_ROWS], F32, name="nobody", tag=slot("z", Z_BANKS))
+            for n in range(WARM):
+                nc.tensor.matmul(out=nobody[:], lhsT=idle[:, 0:PARTS], rhs=idle[:], start=True, stop=True)
+
+        if WARM:
+            op("pe", ("warm", 0), [], warm_up)
         for half in range(2 * HEAD_BLOCKS):
             add_xt(half)
-        op("pe", ("pt", 0), [], transpose_p)
+        op("pe", ("pt", 0), [("casts", 0)], transpose_p)
         for first in range(0, STEPS + T_LAG + GROUP, GROUP):
             ms = [s for s in range(first, first + GROUP) if s < STEPS]
             for s in ms:
-                op("pe", ("m", s), [("xq", s // COL_TILES), ("wq", (s % COL_TILES) // 2)], lambda s=s: multiply(s))
+                op("pe", ("m", s), [("xq", s // COL_TILES), ("wq", piece_of(s % COL_TILES))], lambda s=s: multiply(s))
             ts = [s for s in range(first - T_LAG, first - T_LAG + GROUP) if 0 <= s < STEPS]
             for n, s in enumerate(ts):
                 d = min(first + GROUP - 1, STEPS - 1) if n < DUMMY else None
@@ -365,17 +393,24 @@ def tile_time2vec_t_kernel(tc, x, W, P, w, p, sine_w, cosine_w, out):
                 if first <= x_step(half) < first + GROUP:
                     add_xt(half)
 
-        add_wr(0)
-        add_wq(0)
-        if WQ1_FIRST:
-            if REGROUP[1] == "v":
-                add_wr(1)
-            add_xq(0)
-            add_wq(1)
-        else:
-            add_xq(0)
-        op("v", ("bias", 0), [("pt", 0)], make_bias)
-        wq_at = {WQ_AT[n]: n + 1 for n in range(1 if WQ1_FIRST else 0, 3)}
+        def make_bias_turns():
+            v_affine(bias_turns[:], p_of[0][:, 0:COL_TILES], 1.0 / TWO_PI, on_v["phi_turns"])
+
+        head = {
+            "wr0": lambda: add_wr(0),
+            "wr1": lambda: add_wr(1),
+            "wq0": lambda: add_wq(0),
+            "wq1": lambda: add_wq(1),
+            "xq0a": lambda: op("v", ("xq0", 0), [("xc", 0)], lambda: quantise_x(0, 0, HALF_ROWS)),
+            "xq0b": lambda: op("v", ("xq", 0), [("xc", 1), ("xq0", 0)], lambda: quantise_x(0, HALF_ROWS, BLOCK_ROWS)),
+            "bias_turns": lambda: op("v", ("bias", 0), [("pt", 0)], make_bias_turns),
+        }
+        for name in V_HEAD.split():
+            if name in head:
+                head[name]()
+            else:
+                op("v", ("c", name), [("trig", 0)] if name == "s_sin" else [], chain[name])
+        wq_at = WQ_AT
         v_exit = [STEPS - 2 * n - 2 for n in range(V_EXITS)] + [s for s in range(STEPS - 8) if V_EVERY and s % V_EVERY == V_EVERY - 1]
         for s in range(STEPS + VE_LAG + 1):
             if s < STEPS:
@@ -384,9 +419,9 @@ def tile_time2vec_t_kernel(tc, x, W, P, w, p, sine_w, cosine_w, out):
                 op("v", ("r", s - 1), [("k", s - 1)], lambda s=s: reduce_argument(s - 1))
             if s - VE_LAG in v_exit:
                 op("v", ("e", s - VE_LAG), [("t", s - VE_LAG)] + ([("e", s - VE_LAG - 1)] if (s - VE_LAG) % COL_TILES else []), lambda s=s: leave_psum(s - VE_LAG, "v"))
+            if s == 0:
+                op("v", ("bias2", 0), [], lambda: v_affine(bias[:], bias_turns[:], TWO_PI, None, ALU.mult, ALU.bypass))
             if s in wq_at:
-                if REGROUP[wq_at[s]] == "v":
-                    add_wr(wq_at[s])
                 add_wq(wq_at[s])
             if s == 3:
                 for g in range(1, HEAD_BLOCKS):
@@ -394,19 +429,20 @@ def tile_time2vec_t_kernel(tc, x, W, P, w, p, sine_w, cosine_w, out):
             for half in range(2 * HEAD_BLOCKS, HALVES):
                 if s == x_step(half) + 2 and x_engine(half) == "v":
                     add_xcopy(half)
-                if s == x_step(half) + 4 and half % 2 == 1:
+                if s == x_step(half) + XQ_LAG and half % 2 == 1:
                     add_xq(half // 2)
 
+        op("s", ("trig", 0), [("c", "q")], trig)
         add_xcopy(0)
         add_xcopy(1)
-        for q in range(4):
-            if REGROUP[q] == "s":
-                add_wr(q)
+        for piece in range(len(W_PIECES)):
+            if W_PIECES[piece][2] == "s":
+                add_wr(piece)
         for half in range(2, 2 * HEAD_BLOCKS):
             add_xcopy(half)
         for s in range(STEPS + E_LAG):
             if s < STEPS:
-                op("s", ("sin", s), [("r", s)], lambda s=s: sine(s))
+                op("s", ("sin", s), [("r", s), ("bias2", 0)], lambda s=s: sine(s))
             e = s - E_LAG
             if e >= 0 and e not in v_exit:
                 op("s", ("e", e), [("t", e)] + ([("e", e - 1)] if e % COL_TILES else []), lambda e=e: leave_psum(e, "s"))
@@ -414,9 +450,8 @@ def tile_time2vec_t_kernel(tc, x, W, P, w, p, sine_w, cosine_w, out):
                 if s == x_step(half) + X_COPY_LAG and x_engine(half) == "s":
                     add_xcopy(half)
 
-        for q in range(4):
-            if REGROUP[q] == "g":
-                add_wr(q)
+        op("g", ("casts", 0), [], casts)
+        op("g", ("amp", 0), [("c", "t2"), ("c", "den")], amplitude)
         for g in range(BLOCKS):
             op("g", ("lin", g), [], lambda g=g: linear_term(g))
 

@@ -38,17 +38,20 @@ K_SLOTS = 5
 R_SLOTS = 12
 GROUPED_SLOTS = 2
 OUT_SLOTS = 3
-LIN_SLOTS = 4
+LIN_SLOTS = 2
 LIN_PIECES = 4
 X_AT = 10
 HEAD_BLOCKS = 1
-V_EXITS = 3
+V_TAIL = (58, 60, 62)
 V_EVERY = 0
 VE_LAG = 6
 W_PIECES = ((0, 128, "v"), (128, 256, "v"), (256, 512, "s"), (512, 768, "s"), (768, 1024, "s"))
 X_COPY_LAG = 0
 XQ_LAG = 4
 WARM = 0
+S_GROUP = 1
+TAPER = 0
+GATE = 1
 WQ_AT = {0: 2, 1: 3, 2: 4}
 STORE_STEPS = 4
 FINE_BLOCKS = 1
@@ -139,6 +142,7 @@ def tile_time2vec_t_kernel(tc, x, W, P, w, p, sine_w, cosine_w, out):
         bias_turns = keep.tile([PARTS, COL_TILES], F32, name="bias_turns")
         bias = keep.tile([PARTS, COL_TILES], F32, name="bias")
         p_f32 = keep.tile([PARTS, PARTS], F32, name="p_f32")
+        seen = keep.tile([PARTS, 1], U32, name="seen")
 
         def v_affine(o, i, s1, s2, op0=ALU.mult, op1=ALU.add):
             nc.vector.tensor_scalar(out=o, in0=i, scalar1=s1, scalar2=s2, op0=op0, op1=op1)
@@ -245,15 +249,17 @@ def tile_time2vec_t_kernel(tc, x, W, P, w, p, sine_w, cosine_w, out):
             k_of[s] = k
             v_affine(k[:], z_of[s][:], 1.0 / TWO_PI, bias_turns[:, nt : nt + 1])
 
-        def reduce_argument(s):
-            r = ring.tile([PARTS, BLOCK_ROWS], F32, name="r", tag=slot("r", R_SLOTS))
-            r_of[s] = r
-            v_fused(r[:], k_of[s][:], -TWO_PI, z_of[s][:], ALU.mult, ALU.add)
+        def reduce_argument(s, first=0, after=BLOCK_ROWS):
+            if first == 0:
+                r = ring.tile([PARTS, BLOCK_ROWS], F32, name="r", tag=slot("r", R_SLOTS))
+                r_of[s] = r
+            v_fused(r_of[s][:, first:after], k_of[s][:, first:after], -TWO_PI, z_of[s][:, first:after], ALU.mult, ALU.add)
 
-        def sine(s):
+        def sine(s, first=0, after=BLOCK_ROWS):
             nt = s % COL_TILES
             sine_of[s] = r_of[s]
-            nc.scalar.activation(out=r_of[s][:], in_=r_of[s][:], func=ACT.Sin, bias=bias[:, nt : nt + 1], scale=1.0)
+            part = r_of[s][:, first:after]
+            nc.scalar.activation(out=part, in_=part, func=ACT.Sin, bias=bias[:, nt : nt + 1], scale=1.0)
 
         def open_back(s, dummy_of=None):
             back = psum.tile([PARTS, BLOCK_ROWS], F32, name="back", tag=slot("o", O_BANKS))
@@ -266,6 +272,20 @@ def tile_time2vec_t_kernel(tc, x, W, P, w, p, sine_w, cosine_w, out):
             for j in range(PACK):
                 cols = slice(j * PARTS, (j + 1) * PARTS)
                 nc.tensor.transpose(back[:, cols], sine_of[s][:, cols], ident[:])
+
+        def transpose_piece(s, j):
+            back = psum.tile([PARTS, PARTS], F32, name="piece", tag=slot("o", O_BANKS))
+            back_of[(s, j)] = back
+            nc.tensor.transpose(back[:], sine_of[s][:, j * PARTS : (j + 1) * PARTS], ident[:])
+
+        def leave_piece(s, j, engine):
+            g, nt = divmod(s, COL_TILES)
+            cols = slice(nt * PARTS, (nt + 1) * PARTS)
+            if engine == "v":
+                nc.vector.tensor_scalar(out=out_of[g][:, j, cols], in0=back_of[(s, j)][:], scalar1=on_g["amplitude"], scalar2=None, op0=ALU.mult)
+            else:
+                nc.scalar.activation(out=out_of[g][:, j, cols], in_=back_of[(s, j)][:], func=ACT.Copy, scale=on_g["amplitude"])
+            nc.sync.dma_start(out=out_blocks[g][:, j, K + cols.start : K + cols.stop], in_=out_of[g][:, j, cols])
 
         def leave_psum(s, engine):
             g, nt = divmod(s, COL_TILES)
@@ -386,9 +406,14 @@ def tile_time2vec_t_kernel(tc, x, W, P, w, p, sine_w, cosine_w, out):
             ts = [s for s in range(first - T_LAG, first - T_LAG + GROUP) if 0 <= s < STEPS]
             for n, s in enumerate(ts):
                 d = min(first + GROUP - 1, STEPS - 1) if n < DUMMY else None
-                op("pe", ("ob", s), [], lambda s=s, d=d: open_back(s, d))
+                if s < STEPS - TAPER:
+                    op("pe", ("ob", s), [], lambda s=s, d=d: open_back(s, d))
             for s in ts:
-                op("pe", ("t", s), [("sin", s)], lambda s=s: transpose_back(s))
+                if s < STEPS - TAPER:
+                    op("pe", ("t", s), [("sin", s)], lambda s=s: transpose_back(s))
+                else:
+                    for j in range(PACK):
+                        op("pe", ("tp", s, j), [("sinp", s, j)], lambda s=s, j=j: transpose_piece(s, j))
             for half in range(2 * HEAD_BLOCKS, HALVES):
                 if first <= x_step(half) < first + GROUP:
                     add_xt(half)
@@ -411,12 +436,15 @@ def tile_time2vec_t_kernel(tc, x, W, P, w, p, sine_w, cosine_w, out):
             else:
                 op("v", ("c", name), [("trig", 0)] if name == "s_sin" else [], chain[name])
         wq_at = WQ_AT
-        v_exit = [STEPS - 2 * n - 2 for n in range(V_EXITS)] + [s for s in range(STEPS - 8) if V_EVERY and s % V_EVERY == V_EVERY - 1]
+        v_exit = list(V_TAIL) + [s for s in range(STEPS - 8) if V_EVERY and s % V_EVERY == V_EVERY - 1]
         for s in range(STEPS + VE_LAG + 1):
             if s < STEPS:
                 op("v", ("k", s), [("m", s), ("bias", 0)], lambda s=s: round_turns(s))
-            if 1 <= s <= STEPS:
+            if 1 <= s <= STEPS - TAPER:
                 op("v", ("r", s - 1), [("k", s - 1)], lambda s=s: reduce_argument(s - 1))
+            elif 1 <= s <= STEPS:
+                for j in range(PACK):
+                    op("v", ("rp", s - 1, j), [("k", s - 1)], lambda s=s, j=j: reduce_argument(s - 1, j * PARTS, (j + 1) * PARTS))
             if s - VE_LAG in v_exit:
                 op("v", ("e", s - VE_LAG), [("t", s - VE_LAG)] + ([("e", s - VE_LAG - 1)] if (s - VE_LAG) % COL_TILES else []), lambda s=s: leave_psum(s - VE_LAG, "v"))
             if s == 0:
@@ -440,19 +468,33 @@ def tile_time2vec_t_kernel(tc, x, W, P, w, p, sine_w, cosine_w, out):
                 add_wr(piece)
         for half in range(2, 2 * HEAD_BLOCKS):
             add_xcopy(half)
-        for s in range(STEPS + E_LAG):
-            if s < STEPS:
-                op("s", ("sin", s), [("r", s), ("bias2", 0)], lambda s=s: sine(s))
-            e = s - E_LAG
-            if e >= 0 and e not in v_exit:
-                op("s", ("e", e), [("t", e)] + ([("e", e - 1)] if e % COL_TILES else []), lambda e=e: leave_psum(e, "s"))
+        for base in range(0, STEPS + E_LAG + S_GROUP, S_GROUP):
+            for s in range(base, base + S_GROUP):
+                if s < STEPS - TAPER:
+                    op("s", ("sin", s), [("r", s), ("bias2", 0)], lambda s=s: sine(s))
+                elif s < STEPS:
+                    for j in range(PACK):
+                        op("s", ("sinp", s, j), [("rp", s, j)], lambda s=s, j=j: sine(s, j * PARTS, (j + 1) * PARTS))
+            for e in range(base - E_LAG, base - E_LAG + S_GROUP):
+                if 0 <= e < STEPS - TAPER and e not in v_exit:
+                    op("s", ("e", e), [("t", e)] + ([("e", e - 1)] if e % COL_TILES else []), lambda e=e: leave_psum(e, "s"))
+                elif STEPS - TAPER <= e < STEPS:
+                    for j in range(PACK):
+                        op("s", ("ep", e, j), [("tp", e, j), ("e", STEPS - TAPER - 1)], lambda e=e, j=j: leave_piece(e, j, "s"))
             for half in range(2 * HEAD_BLOCKS, HALVES):
-                if s == x_step(half) + X_COPY_LAG and x_engine(half) == "s":
+                if base <= x_step(half) + X_COPY_LAG < base + S_GROUP and x_engine(half) == "s":
                     add_xcopy(half)
 
         op("g", ("casts", 0), [], casts)
         op("g", ("amp", 0), [("c", "t2"), ("c", "den")], amplitude)
+        def stand_behind(codes):
+            nc.gpsimd.tensor_copy(out=seen[:], in_=codes)
+
         for g in range(BLOCKS):
+            if GATE and g == 0:
+                op("g", ("gate", g), [("wq", len(W_PIECES) - 1)], lambda: stand_behind(w_codes[:, N - 1 : N]))
+            elif GATE:
+                op("g", ("gate", g), [("xq", g)], lambda g=g: stand_behind(x_codes[g][:, 0:1]))
             op("g", ("lin", g), [], lambda g=g: linear_term(g))
 
         done = set()

@@ -31,7 +31,7 @@ GROUP = 2
 Z_BANKS = 4
 O_BANKS = 4
 X_RING = "o"
-T_LAG = 5
+T_LAG = 4
 E_LAG = 3
 DUMMY = 0
 K_SLOTS = 5
@@ -42,7 +42,7 @@ LIN_SLOTS = 2
 LIN_PIECES = 4
 X_AT = 10
 HEAD_BLOCKS = 1
-V_TAIL = (58, 60, 62)
+V_TAIL = (60, 62)
 V_EVERY = 0
 VE_LAG = 6
 W_PIECES = ((0, 128, "v"), (128, 256, "v"), (256, 512, "s"), (512, 768, "s"), (768, 1024, "s"))
@@ -52,6 +52,8 @@ WARM = 0
 S_GROUP = 1
 TAPER = 0
 GATE = 1
+TAIL_FROM = 0
+E_LAG_TAIL = 2
 WQ_AT = {0: 2, 1: 3, 2: 4}
 STORE_STEPS = 4
 FINE_BLOCKS = 1
@@ -475,7 +477,7 @@ def tile_time2vec_t_kernel(tc, x, W, P, w, p, sine_w, cosine_w, out):
                 elif s < STEPS:
                     for j in range(PACK):
                         op("s", ("sinp", s, j), [("rp", s, j)], lambda s=s, j=j: sine(s, j * PARTS, (j + 1) * PARTS))
-            for e in range(base - E_LAG, base - E_LAG + S_GROUP):
+            for e in [e for e in range(STEPS) if base <= e + (E_LAG if e < TAIL_FROM else E_LAG_TAIL) < base + S_GROUP]:
                 if 0 <= e < STEPS - TAPER and e not in v_exit:
                     op("s", ("e", e), [("t", e)] + ([("e", e - 1)] if e % COL_TILES else []), lambda e=e: leave_psum(e, "s"))
                 elif STEPS - TAPER <= e < STEPS:

@@ -40,14 +40,14 @@ GROUPED_SLOTS = 2
 OUT_SLOTS = 3
 LIN_SLOTS = 2
 LIN_PIECES = 4
-X_AT = 10
+X_AT = 14
 HEAD_BLOCKS = 1
 V_TAIL = (60, 62)
 V_EVERY = 0
 VE_LAG = 6
 W_PIECES = ((0, 128, "v"), (128, 256, "v"), (256, 512, "s"), (512, 768, "s"), (768, 1024, "s"))
 X_COPY_LAG = 0
-XQ_LAG = 4
+XQ_LAG = 6
 WARM = 0
 S_GROUP = 1
 TAPER = 0

import math
from contextlib import ExitStack

import concourse.mybir as mybir
from concourse.masks import make_identity

FLOPS = 2 * 4096 * 512 * 1024

F32 = mybir.dt.float32
BF16 = mybir.dt.bfloat16
I32 = mybir.dt.int32
U32 = mybir.dt.uint32
U8 = mybir.dt.uint8
FP8X4 = mybir.dt.float8_e4m3fn_x4
ALU = mybir.AluOpType
ACT = mybir.ActivationFunctionType

PARTS = 128
PACK = 4
K = 512
N = 1024
BLOCK_ROWS = PARTS * PACK
BLOCKS = 4096 // BLOCK_ROWS
HALVES = 2 * BLOCKS
HALF_ROWS = BLOCK_ROWS // 2
COL_TILES = N // PARTS
STEPS = BLOCKS * COL_TILES
W_QUARTER = N // 4

GROUP = 2
Z_BANKS = 4
O_BANKS = 4
X_RING = "o"
T_LAG = 4
E_LAG = 3
DUMMY = 0
K_SLOTS = 5
R_SLOTS = 12
GROUPED_SLOTS = 2
OUT_SLOTS = 3
LIN_SLOTS = 2
LIN_PIECES = 4
X_AT = 14
HEAD_BLOCKS = 1
V_TAIL = (60, 62)
V_EVERY = 0
VE_LAG = 6
W_PIECES = ((0, 128, "v"), (128, 256, "v"), (256, 512, "s"), (512, 768, "s"), (768, 1024, "s"))
X_COPY_LAG = 0
XQ_LAG = 6
WARM = 0
S_GROUP = 1
TAPER = 0
GATE = 1
TAIL_FROM = 0
E_LAG_TAIL = 2
WQ_AT = {0: 2, 1: 3, 2: 4}
STORE_STEPS = 4
FINE_BLOCKS = 1
XCOPY_V = 0

V_HEAD = (
    "c_abs s_abs s half_sign sum inv_sum q sign_turns wr0 theta0 s_sin c_sin num den wq0 inv_den wr1 t xq0a t2 t_turns "
    "theta0_turns high t4 low series xq0b phi_turns bias_turns wq1"
)

TWO_PI = 2.0 * math.pi
HALF_PI = 0.5 * math.pi
TINY = 1.0e-30


def tile_time2vec_t_kernel(tc, x, W, P, w, p, sine_w, cosine_w, out):
    nc = tc.nc
    with ExitStack() as ctx:
        keep = ctx.enter_context(tc.tile_pool(name="keep", bufs=1))
        ring = ctx.enter_context(tc.tile_pool(name="ring", bufs=1))
        psum = ctx.enter_context(tc.psum_pool(name="psum", bufs=1))
        ctx.enter_context(tc.manual_schedule())

        taken = {}

        def slot(kind, slots):
            n = taken.get(kind, 0)
            taken[kind] = n + 1
            return "%s%d" % (kind, n % slots)

        x_blocks = x.rearrange("(g p j) k -> g p j k", p=PARTS, j=PACK)
        out_blocks = out.rearrange("(g p j) m -> g p j m", p=PARTS, j=PACK)
        w_rows = W.rearrange("(p t) n -> p t n", t=PACK)

        c_bf = keep.tile([PARTS, 1], BF16, name="c_bf")
        s_bf = keep.tile([PARTS, 1], BF16, name="s_bf")
        w_bf = keep.tile([PARTS, 1], BF16, name="w_bf")
        p_bf = keep.tile([PARTS, 1], BF16, name="p_bf")
        p_rows = keep.tile([PARTS, PARTS], BF16, name="p_rows")
        zero = keep.tile([PARTS, 1], F32, name="zero")
        unused = keep.tile([PARTS, 1], F32, name="unused")
        nc.vector.memset(p_rows[:], 0.0)
        if WARM:
            idle = keep.tile([PARTS, BLOCK_ROWS], BF16, name="idle")
            nc.vector.memset(idle[:], 0.0)
        nc.vector.memset(zero[:], 0.0)

        nc.scalar.dma_start(out=c_bf[:], in_=cosine_w.partition_broadcast(PARTS))
        nc.sync.dma_start(out=s_bf[:], in_=sine_w.partition_broadcast(PARTS))
        nc.scalar.dma_start(out=p_rows[0:COL_TILES, :], in_=P.rearrange("(t n) -> t n", n=PARTS))

        x_sb = [keep.tile([PARTS, PACK, K], BF16, name="x_sb%d" % g) for g in range(BLOCKS)]
        w_raw = keep.tile([PARTS, PACK, N], BF16, name="w_raw")

        def load_w(q):
            cols = slice(q * W_QUARTER, (q + 1) * W_QUARTER)
            nc.sync.dma_start(out=w_raw[:, :, cols], in_=w_rows[:, :, cols])

        nc.sync.dma_start(out=x_sb[0][:, 0:2, :], in_=x_blocks[0][:, 0:2, :])
        load_w(0)
        nc.sync.dma_start(out=x_sb[0][:, 2:4, :], in_=x_blocks[0][:, 2:4, :])
        load_w(1)
        load_w(2)
        load_w(3)
        for g in range(1, BLOCKS):
            nc.sync.dma_start(out=x_sb[g][:], in_=x_blocks[g])
            if g == 1:
                nc.sync.dma_start(out=w_bf[:], in_=w.partition_broadcast(PARTS))
                nc.sync.dma_start(out=p_bf[:], in_=p.partition_broadcast(PARTS))

        nc.scalar.activation(out=unused[:], in_=zero[:], func=ACT.Sin)

        ident = keep.tile([PARTS, PARTS], F32, name="ident")
        make_identity(nc, ident[:])

        v_names = (
            "c_abs", "s_abs", "half_sign", "s", "sum", "inv_sum", "q", "theta0", "s_sin", "c_sin", "num", "den",
            "inv_den", "t", "t2", "t4", "low", "high", "series", "sign_turns", "theta0_turns", "t_turns", "phi_turns",
        )
        g_names = ("root1", "root2", "root3", "amplitude", "w", "p")
        v_tile = keep.tile([PARTS, len(v_names)], F32, name="v_tile")
        g_tile = keep.tile([PARTS, len(g_names)], F32, name="g_tile")
        trig = keep.tile([PARTS, 2], F32, name="trig")
        on_v = {name: v_tile[:, i : i + 1] for i, name in enumerate(v_names)}
        on_g = {name: g_tile[:, i : i + 1] for i, name in enumerate(g_names)}
        sin0 = trig[:, 0:1]
        cos0 = trig[:, 1:2]
        bias_turns = keep.tile([PARTS, COL_TILES], F32, name="bias_turns")
        bias = keep.tile([PARTS, COL_TILES], F32, name="bias")
        p_f32 = keep.tile([PARTS, PARTS], F32, name="p_f32")
        seen = keep.tile([PARTS, 1], U32, name="seen")

        def v_affine(o, i, s1, s2, op0=ALU.mult, op1=ALU.add):
            nc.vector.tensor_scalar(out=o, in0=i, scalar1=s1, scalar2=s2, op0=op0, op1=op1)

        def v_fused(o, i0, s, i1, op0, op1):
            nc.vector.scalar_tensor_tensor(out=o, in0=i0, scalar=s, in1=i1, op0=op0, op1=op1)

        def v_mul(o, i0, i1):
            nc.vector.tensor_tensor(out=o, in0=i0, in1=i1, op=ALU.mult)

        def g_affine(o, i, s1, s2):
            nc.gpsimd.tensor_scalar(out=o, in0=i, scalar1=s1, scalar2=s2, op0=ALU.mult, op1=ALU.add)

        w_grouped = keep.tile([PARTS, N, PACK], BF16, name="w_grouped", align_bytes=64)
        w_codes = keep.tile([PARTS, N], U32, name="w_codes", align_bytes=64)
        w_scales = keep.tile([PARTS, N], U8, name="w_scales", align_bytes=64)

        def regroup_w(piece):
            first, after, engine = W_PIECES[piece]
            dst = w_grouped[:, first:after, :].rearrange("p (c i) t -> p c t i", i=4)
            src = w_raw[:, :, first:after].rearrange("p t (c i) -> p c t i", i=4)
            if engine == "s":
                nc.scalar.copy(out=dst, in_=src)
            else:
                nc.vector.tensor_copy(out=dst, in_=src)

        def quantise_w(piece):
            first, after, engine = W_PIECES[piece]
            nc.vector.quantize_mx(
                out=w_codes[:, first:after].bitcast(FP8X4),
                scales=w_scales[:, first:after],
                in_=w_grouped[:, first:after, :].rearrange("p c t -> p (c t)"),
            )

        x_t = {}
        x_grouped = {}
        x_codes = {}
        x_scales = {}

        def transpose_x(half):
            g, h = divmod(half, 2)
            words = x_sb[g][:].bitcast(F32).rearrange("p j (q u) -> p j q u", u=2)
            banks = {"o": O_BANKS, "z": Z_BANKS, "x": 1}[X_RING]
            planes = psum.tile([PARTS, 2, HALF_ROWS], F32, name="planes", tag=slot(X_RING, banks))
            x_t[half] = planes
            for jj in range(2):
                for u in range(2):
                    nc.tensor.transpose(planes[:, u, jj * PARTS : (jj + 1) * PARTS], words[:, 2 * h + jj, :, u], ident[:])

        def copy_x(half, engine):
            g, h = divmod(half, 2)
            if h == 0:
                grouped = ring.tile(
                    [PARTS, BLOCK_ROWS, PACK], BF16, name="grouped", tag=slot("grouped", GROUPED_SLOTS), align_bytes=64
                )
                x_grouped[g] = grouped
            dst = x_grouped[g][:].bitcast(F32)[:, h * HALF_ROWS : (h + 1) * HALF_ROWS, :]
            src = x_t[half][:].rearrange("p u c -> p c u")
            if engine == "s":
                nc.scalar.copy(out=dst, in_=src)
            else:
                nc.vector.tensor_copy(out=dst, in_=src)

        def quantise_x(g, first=0, after=BLOCK_ROWS):
            if first == 0:
                codes = keep.tile([PARTS, BLOCK_ROWS], U32, name="codes%d" % g, align_bytes=64)
                scales = keep.tile([PARTS, BLOCK_ROWS], U8, name="scales%d" % g, align_bytes=64)
                x_codes[g] = codes
                x_scales[g] = scales
            nc.vector.quantize_mx(
                out=x_codes[g][:, first:after].bitcast(FP8X4),
                scales=x_scales[g][:, first:after],
                in_=x_grouped[g][:, first:after, :].rearrange("p c t -> p (c t)"),
            )

        z_of = {}
        k_of = {}
        r_of = {}
        sine_of = {}
        back_of = {}
        out_of = {}

        def pass_mx(dst, s):
            g, nt = divmod(s, COL_TILES)
            cols = slice(nt * PARTS, (nt + 1) * PARTS)
            nc.tensor.matmul_mx(
                out=dst,
                lhsT=w_codes[:, cols].bitcast(FP8X4),
                lhsT_scale=w_scales[:, cols],
                rhs=x_codes[g][:].bitcast(FP8X4),
                rhs_scale=x_scales[g][:],
                start=True,
                stop=True,
            )

        def multiply(s):
            z = psum.tile([PARTS, BLOCK_ROWS], F32, name="z", tag=slot("z", Z_BANKS))
            z_of[s] = z
            pass_mx(z[:], s)

        def round_turns(s):
            nt = s % COL_TILES
            k = ring.tile([PARTS, BLOCK_ROWS], I32, name="k", tag=slot("k", K_SLOTS))
            k_of[s] = k
            v_affine(k[:], z_of[s][:], 1.0 / TWO_PI, bias_turns[:, nt : nt + 1])

        def reduce_argument(s, first=0, after=BLOCK_ROWS):
            if first == 0:
                r = ring.tile([PARTS, BLOCK_ROWS], F32, name="r", tag=slot("r", R_SLOTS))
                r_of[s] = r
            v_fused(r_of[s][:, first:after], k_of[s][:, first:after], -TWO_PI, z_of[s][:, first:after], ALU.mult, ALU.add)

        def sine(s, first=0, after=BLOCK_ROWS):
            nt = s % COL_TILES
            sine_of[s] = r_of[s]
            part = r_of[s][:, first:after]
            nc.scalar.activation(out=part, in_=part, func=ACT.Sin, bias=bias[:, nt : nt + 1], scale=1.0)

        def open_back(s, dummy_of=None):
            back = psum.tile([PARTS, BLOCK_ROWS], F32, name="back", tag=slot("o", O_BANKS))
            back_of[s] = back
            if dummy_of is not None:
                pass_mx(back[:], dummy_of)

        def transpose_back(s):
            back = back_of[s]
            for j in range(PACK):
                cols = slice(j * PARTS, (j + 1) * PARTS)
                nc.tensor.transpose(back[:, cols], sine_of[s][:, cols], ident[:])

        def transpose_piece(s, j):
            back = psum.tile([PARTS, PARTS], F32, name="piece", tag=slot("o", O_BANKS))
            back_of[(s, j)] = back
            nc.tensor.transpose(back[:], sine_of[s][:, j * PARTS : (j + 1) * PARTS], ident[:])

        def leave_piece(s, j, engine):
            g, nt = divmod(s, COL_TILES)
            cols = slice(nt * PARTS, (nt + 1) * PARTS)
            if engine == "v":
                nc.vector.tensor_scalar(out=out_of[g][:, j, cols], in0=back_of[(s, j)][:], scalar1=on_g["amplitude"], scalar2=None, op0=ALU.mult)
            else:
                nc.scalar.activation(out=out_of[g][:, j, cols], in_=back_of[(s, j)][:], func=ACT.Copy, scale=on_g["amplitude"])
            nc.sync.dma_start(out=out_blocks[g][:, j, K + cols.start : K + cols.stop], in_=out_of[g][:, j, cols])

        def leave_psum(s, engine):
            g, nt = divmod(s, COL_TILES)
            if nt == 0:
                tile_out = ring.tile([PARTS, PACK, N], F32, name="tile_out", tag=slot("out", OUT_SLOTS))
                out_of[g] = tile_out
            dst = out_of[g][:, :, nt * PARTS : (nt + 1) * PARTS]
            src = back_of[s][:].rearrange("p (j n) -> p j n", j=PACK)
            if engine == "v":
                nc.vector.tensor_scalar(out=dst, in0=src, scalar1=on_g["amplitude"], scalar2=None, op0=ALU.mult)
            else:
                nc.scalar.activation(out=dst, in_=src, func=ACT.Copy, scale=on_g["amplitude"])
            unit = 1 if g >= BLOCKS - FINE_BLOCKS else STORE_STEPS
            if (nt + 1) % unit == 0:
                cols = slice((nt + 1 - unit) * PARTS, (nt + 1) * PARTS)
                nc.sync.dma_start(out=out_blocks[g][:, :, K + cols.start : K + cols.stop], in_=out_of[g][:, :, cols])

        def linear_term(g):
            lin = ring.tile([PARTS, PACK, K], F32, name="lin", tag=slot("lin", LIN_SLOTS))
            for j in range(LIN_PIECES):
                a, b = j * PACK // LIN_PIECES, (j + 1) * PACK // LIN_PIECES
                g_affine(lin[:, a:b, :], x_sb[g][:, a:b, :], on_g["w"], on_g["p"])
            nc.gpsimd.dma_start(out=out_blocks[g][:, :, 0:K], in_=lin[:])

        chain = {
            "c_abs": lambda: v_fused(on_v["c_abs"], c_bf[:], -1.0, c_bf[:], ALU.mult, ALU.max),
            "s_abs": lambda: v_fused(on_v["s_abs"], s_bf[:], -1.0, s_bf[:], ALU.mult, ALU.max),
            "s": lambda: nc.vector.tensor_copy(out=on_v["s"], in_=s_bf[:]),
            "half_sign": lambda: v_affine(on_v["half_sign"], c_bf[:], 0.0, 0.5, ALU.is_ge, ALU.subtract),
            "sum": lambda: v_fused(on_v["sum"], on_v["s_abs"], TINY, on_v["c_abs"], ALU.max, ALU.add),
            "inv_sum": lambda: nc.vector.reciprocal(out=on_v["inv_sum"], in_=on_v["sum"]),
            "q": lambda: v_mul(on_v["q"], on_v["s"], on_v["inv_sum"]),
            "theta0": lambda: v_affine(on_v["theta0"], on_v["q"], -HALF_PI, HALF_PI),
            "sign_turns": lambda: v_affine(on_v["sign_turns"], on_v["half_sign"], 1.0 / math.pi, None, ALU.mult, ALU.bypass),
            "theta0_turns": lambda: v_mul(on_v["theta0_turns"], on_v["theta0"], on_v["sign_turns"]),
            "s_sin": lambda: v_affine(on_v["s_sin"], sin0, on_v["s"], None, ALU.mult, ALU.bypass),
            "c_sin": lambda: v_affine(on_v["c_sin"], sin0, on_v["c_abs"], TINY, ALU.mult, ALU.max),
            "num": lambda: v_fused(on_v["num"], cos0, on_v["c_abs"], on_v["s_sin"], ALU.mult, ALU.subtract),
            "den": lambda: v_fused(on_v["den"], cos0, on_v["s"], on_v["c_sin"], ALU.mult, ALU.add),
            "inv_den": lambda: nc.vector.reciprocal(out=on_v["inv_den"], in_=on_v["den"]),
            "t": lambda: v_mul(on_v["t"], on_v["num"], on_v["inv_den"]),
            "t2": lambda: v_mul(on_v["t2"], on_v["t"], on_v["t"]),
            "t_turns": lambda: v_mul(on_v["t_turns"], on_v["t"], on_v["sign_turns"]),
            "high": lambda: v_affine(on_v["high"], on_v["t2"], -1.0 / 7.0, 0.2),
            "t4": lambda: v_mul(on_v["t4"], on_v["t2"], on_v["t2"]),
            "low": lambda: v_affine(on_v["low"], on_v["t2"], -1.0 / 3.0, 1.0),
            "series": lambda: v_affine(on_v["series"], on_v["high"], on_v["t4"], on_v["low"]),
            "phi_turns": lambda: v_affine(on_v["phi_turns"], on_v["series"], on_v["t_turns"], on_v["theta0_turns"]),
        }

        def trig():
            nc.scalar.activation(out=cos0, in_=on_v["q"], func=ACT.Sin, scale=HALF_PI)
            nc.scalar.activation(out=sin0, in_=on_v["q"], func=ACT.Sin, scale=-HALF_PI, bias=HALF_PI)

        def casts():
            nc.gpsimd.tensor_copy(out=p_f32[:], in_=p_rows[:])

        def amplitude():
            g_affine(on_g["root1"], on_v["t2"], 1.0 / 16.0, -0.125)
            g_affine(on_g["root2"], on_g["root1"], on_v["t2"], 0.5)
            g_affine(on_g["root3"], on_g["root2"], on_v["t2"], 1.0)
            nc.gpsimd.tensor_tensor(out=on_g["amplitude"], in0=on_g["root3"], in1=on_v["den"], op=ALU.mult)
            nc.gpsimd.tensor_copy(out=on_g["w"], in_=w_bf[:])
            nc.gpsimd.tensor_copy(out=on_g["p"], in_=p_bf[:])

        prog = {"pe": [], "v": [], "s": [], "g": []}

        def op(engine, key, needs, emit):
            prog[engine].append((key, needs, emit))

        def x_engine(half):
            return "v" if half >= 2 * HEAD_BLOCKS and XCOPY_V and half % XCOPY_V == 1 else "s"

        def add_xt(half):
            op("pe", ("xt", half), [], lambda: transpose_x(half))

        def add_xcopy(half):
            e = x_engine(half)
            needs = [("xt", half)] + ([("xc", half - 1)] if half % 2 else [])
            op(e, ("xc", half), needs, lambda: copy_x(half, e))

        def add_xq(g):
            op("v", ("xq", g), [("xc", 2 * g), ("xc", 2 * g + 1)], lambda: quantise_x(g))

        def add_wq(piece):
            op("v", ("wq", piece), [("wr", piece)], lambda: quantise_w(piece))

        def add_wr(piece):
            op(W_PIECES[piece][2], ("wr", piece), [], lambda: regroup_w(piece))

        def piece_of(nt):
            return [n for n, piece in enumerate(W_PIECES) if piece[0] <= nt * PARTS < piece[1]][0]

        p_of = {}

        def transpose_p():
            p_t = psum.tile([PARTS, PARTS], F32, name="p_t", tag=slot("z", Z_BANKS))
            p_of[0] = p_t
            nc.tensor.transpose(p_t[:], p_f32[:], ident[:])

        def x_step(half):
            return max(0, 4 * half - X_AT)

        def warm_up():
            nobody = psum.tile([PARTS, BLOCK_ROWS], F32, name="nobody", tag=slot("z", Z_BANKS))
            for n in range(WARM):
                nc.tensor.matmul(out=nobody[:], lhsT=idle[:, 0:PARTS], rhs=idle[:], start=True, stop=True)

        if WARM:
            op("pe", ("warm", 0), [], warm_up)
        for half in range(2 * HEAD_BLOCKS):
            add_xt(half)
        op("pe", ("pt", 0), [("casts", 0)], transpose_p)
        for first in range(0, STEPS + T_LAG + GROUP, GROUP):
            ms = [s for s in range(first, first + GROUP) if s < STEPS]
            for s in ms:
                op("pe", ("m", s), [("xq", s // COL_TILES), ("wq", piece_of(s % COL_TILES))], lambda s=s: multiply(s))
            ts = [s for s in range(first - T_LAG, first - T_LAG + GROUP) if 0 <= s < STEPS]
            for n, s in enumerate(ts):
                d = min(first + GROUP - 1, STEPS - 1) if n < DUMMY else None
                if s < STEPS - TAPER:
                    op("pe", ("ob", s), [], lambda s=s, d=d: open_back(s, d))
            for s in ts:
                if s < STEPS - TAPER:
                    op("pe", ("t", s), [("sin", s)], lambda s=s: transpose_back(s))
                else:
                    for j in range(PACK):
                        op("pe", ("tp", s, j), [("sinp", s, j)], lambda s=s, j=j: transpose_piece(s, j))
            for half in range(2 * HEAD_BLOCKS, HALVES):
                if first <= x_step(half) < first + GROUP:
                    add_xt(half)

        def make_bias_turns():
            v_affine(bias_turns[:], p_of[0][:, 0:COL_TILES], 1.0 / TWO_PI, on_v["phi_turns"])

        head = {
            "wr0": lambda: add_wr(0),
            "wr1": lambda: add_wr(1),
            "wq0": lambda: add_wq(0),
            "wq1": lambda: add_wq(1),
            "xq0a": lambda: op("v", ("xq0", 0), [("xc", 0)], lambda: quantise_x(0, 0, HALF_ROWS)),
            "xq0b": lambda: op("v", ("xq", 0), [("xc", 1), ("xq0", 0)], lambda: quantise_x(0, HALF_ROWS, BLOCK_ROWS)),
            "bias_turns": lambda: op("v", ("bias", 0), [("pt", 0)], make_bias_turns),
        }
        for name in V_HEAD.split():
            if name in head:
                head[name]()
            else:
                op("v", ("c", name), [("trig", 0)] if name == "s_sin" else [], chain[name])
        wq_at = WQ_AT
        v_exit = list(V_TAIL) + [s for s in range(STEPS - 8) if V_EVERY and s % V_EVERY == V_EVERY - 1]
        for s in range(STEPS + VE_LAG + 1):
            if s < STEPS:
                op("v", ("k", s), [("m", s), ("bias", 0)], lambda s=s: round_turns(s))
            if 1 <= s <= STEPS - TAPER:
                op("v", ("r", s - 1), [("k", s - 1)], lambda s=s: reduce_argument(s - 1))
            elif 1 <= s <= STEPS:
                for j in range(PACK):
                    op("v", ("rp", s - 1, j), [("k", s - 1)], lambda s=s, j=j: reduce_argument(s - 1, j * PARTS, (j + 1) * PARTS))
            if s - VE_LAG in v_exit:
                op("v", ("e", s - VE_LAG), [("t", s - VE_LAG)] + ([("e", s - VE_LAG - 1)] if (s - VE_LAG) % COL_TILES else []), lambda s=s: leave_psum(s - VE_LAG, "v"))
            if s == 0:
                op("v", ("bias2", 0), [], lambda: v_affine(bias[:], bias_turns[:], TWO_PI, None, ALU.mult, ALU.bypass))
            if s in wq_at:
                add_wq(wq_at[s])
            if s == 3:
                for g in range(1, HEAD_BLOCKS):
                    add_xq(g)
            for half in range(2 * HEAD_BLOCKS, HALVES):
                if s == x_step(half) + 2 and x_engine(half) == "v":
                    add_xcopy(half)
                if s == x_step(half) + XQ_LAG and half % 2 == 1:
                    add_xq(half // 2)

        op("s", ("trig", 0), [("c", "q")], trig)
        add_xcopy(0)
        add_xcopy(1)
        for piece in range(len(W_PIECES)):
            if W_PIECES[piece][2] == "s":
                add_wr(piece)
        for half in range(2, 2 * HEAD_BLOCKS):
            add_xcopy(half)
        for base in range(0, STEPS + E_LAG + S_GROUP, S_GROUP):
            for s in range(base, base + S_GROUP):
                if s < STEPS - TAPER:
                    op("s", ("sin", s), [("r", s), ("bias2", 0)], lambda s=s: sine(s))
                elif s < STEPS:
                    for j in range(PACK):
                        op("s", ("sinp", s, j), [("rp", s, j)], lambda s=s, j=j: sine(s, j * PARTS, (j + 1) * PARTS))
            for e in [e for e in range(STEPS) if base <= e + (E_LAG if e < TAIL_FROM else E_LAG_TAIL) < base + S_GROUP]:
                if 0 <= e < STEPS - TAPER and e not in v_exit:
                    op("s", ("e", e), [("t", e)] + ([("e", e - 1)] if e % COL_TILES else []), lambda e=e: leave_psum(e, "s"))
                elif STEPS - TAPER <= e < STEPS:
                    for j in range(PACK):
                        op("s", ("ep", e, j), [("tp", e, j), ("e", STEPS - TAPER - 1)], lambda e=e, j=j: leave_piece(e, j, "s"))
            for half in range(2 * HEAD_BLOCKS, HALVES):
                if base <= x_step(half) + X_COPY_LAG < base + S_GROUP and x_engine(half) == "s":
                    add_xcopy(half)

        op("g", ("casts", 0), [], casts)
        op("g", ("amp", 0), [("c", "t2"), ("c", "den")], amplitude)
        def stand_behind(codes):
            nc.gpsimd.tensor_copy(out=seen[:], in_=codes)

        for g in range(BLOCKS):
            if GATE and g == 0:
                op("g", ("gate", g), [("wq", len(W_PIECES) - 1)], lambda: stand_behind(w_codes[:, N - 1 : N]))
            elif GATE:
                op("g", ("gate", g), [("xq", g)], lambda g=g: stand_behind(x_codes[g][:, 0:1]))
            op("g", ("lin", g), [], lambda g=g: linear_term(g))

        done = set()
        at = {e: 0 for e in prog}
        total = sum(len(v) for v in prog.values())
        for turn in range(total):
            for e in ("pe", "v", "s", "g"):
                for n in range(3 * GROUP + 2 if e == "pe" else 1):
                    if at[e] < len(prog[e]) and all(need in done for need in prog[e][at[e]][1]):
                        prog[e][at[e]][2]()
                        done.add(prog[e][at[e]][0])
                        at[e] += 1
        assert len(done) == total, "the programs wait for each other"
